import numpy as np
import ml_dtypes


def mxq(x, axis, fmt="e4m3"):
    dtype, down = {"e4m3": (ml_dtypes.float8_e4m3fn, 7), "e5m2": (ml_dtypes.float8_e5m2, 14)}[fmt]
    v = np.moveaxis(np.asarray(x, np.float32).astype(ml_dtypes.bfloat16).astype(np.float64), axis, -1)
    blocks = v.reshape(v.shape[:-1] + (-1, 32))
    amax = np.abs(blocks).max(-1, keepdims=True)
    byte = np.maximum(np.where(amax > 0, np.frexp(amax)[1] - 1 + 127, 0) - down, 1)
    scale = np.exp2(byte - 127.0)
    codes = (blocks / scale).astype(np.float32).astype(dtype).astype(np.float64)
    return np.moveaxis((codes * scale).reshape(v.shape), -1, axis)


WIDE = False


def mx_kscale(k):
    if not WIDE:
        return np.ones(k)
    levels = np.array([10, -10, 5, -5, 0])
    a = np.random.permutation(np.resize(levels, k // 512 * 4)).reshape(k // 512, 4)
    idx = np.arange(k)
    return np.exp2(a[idx // 512, idx % 128 // 32])


BF16 = ml_dtypes.bfloat16


def bf(x):
    return np.asarray(x, np.float32).astype(BF16)


def f64(x):
    return np.asarray(x).astype(np.float64)


B, HQ, HK, S, D, HID, BS = 1, 8, 2, 4096, 256, 512, 8
NB = S // BS
G = HQ // HK


def rotate_half(x):
    h = x.shape[-1] // 2
    return np.concatenate([-x[..., h:], x[..., :h]], axis=-1)


def pool_cat(x):
    b, h, s, d = x.shape
    xb = x.reshape(b, h, s // BS, BS, d)
    return np.concatenate([xb.mean(axis=3), xb.max(axis=3)], axis=-1)


def setup_inputs():
    s = mx_kscale(2 * D)[:D]
    s2 = np.concatenate([s, s])
    t = mx_kscale(HID)[:HID // 2]
    t2 = np.concatenate([t, t])
    q = bf(np.random.standard_normal((B, HQ, S, D)) * s)
    k = bf(np.random.standard_normal((B, HK, S, D)) * s)
    wq = bf(np.random.standard_normal((HQ, 2 * D, HID)) * 1.25 / np.sqrt(2 * D) / s2[:, None] * t2)
    wk = bf(np.random.standard_normal((HK, 2 * D, HID)) * 1.25 / np.sqrt(2 * D) / s2[:, None] / t2)
    keep = np.random.random((B, 1, NB, NB)) < 0.9
    mask = np.tril(np.ones((NB, NB), bool), 1) & (keep | np.eye(NB, dtype=bool) | np.eye(NB, k=1, dtype=bool))
    pos = np.arange(NB, dtype=np.float64)
    inv_freq = 1.0 / (10000.0 ** (np.arange(0, HID, 2, dtype=np.float64) / HID))
    freqs = pos[:, None] * inv_freq[None, :]
    emb = np.concatenate([freqs, freqs], axis=-1)
    cos = bf(np.broadcast_to(np.cos(emb)[None], (B, NB, HID)))
    sin = bf(np.broadcast_to(np.sin(emb)[None], (B, NB, HID)))
    return {"q": q, "k": k, "attention_mask": mask, "cos": cos, "sin": sin, "wq": wq, "wk": wk}


def reference(q, k, attention_mask, cos, sin, wq, wk):
    qh = mxq(pool_cat(f64(q)), 3, "e4m3") @ mxq(f64(wq), 1, "e4m3")
    kh = mxq(pool_cat(f64(k)), 3, "e4m3") @ mxq(f64(wk), 1, "e4m3")
    c, s = f64(cos)[:, None], f64(sin)[:, None]
    qh = qh * c + rotate_half(qh) * s
    kh = kh * c + rotate_half(kh) * s
    qg = qh.reshape(B, HK, G * NB, HID)
    attn = (mxq(qg, 3, "e4m3") @ mxq(kh.transpose(0, 1, 3, 2), 2, "e4m3")).reshape(B, HQ, NB, NB) / np.sqrt(HID)
    attn = np.where(attention_mask, attn, -1e9)
    e = np.exp(attn - attn.max(axis=-1, keepdims=True))
    return e / e.sum(axis=-1, keepdims=True)

@@ -1,0 +1,346 @@
+import math
+from contextlib import ExitStack
+
+import concourse.mybir as mybir
+from concourse.masks import make_identity
+
+FP8X4 = mybir.dt.float8_e4m3fn_x4
+BF16 = mybir.dt.bfloat16
+F32 = mybir.dt.float32
+I32 = mybir.dt.int32
+U32 = mybir.dt.uint32
+U8 = mybir.dt.uint8
+ALU = mybir.AluOpType
+ACT = mybir.ActivationFunctionType
+AX = mybir.AxisListType
+
+P = 128
+HQ, HK, S, D, HID, BS = 8, 2, 4096, 256, 512, 8
+NB = S // BS
+G = HQ // HK
+HB = NB // 2
+FLOPS = 2 * NB * (2 * D) * HID * (HQ + HK) + 2 * NB * NB * HID * HQ
+SCALE = 1.0 / math.sqrt(HID)
+MANUAL = False
+ADD_ON_G = True
+
+
+def tile_attngate_kernel(tc, q, k, attention_mask, cos, sin, wq, wk, out):
+    nc = tc.nc
+    streams = []
+    for kv in range(HK):
+        streams.append((k[0, kv], wk[kv], kv, None))
+        for gq in range(G):
+            streams.append((q[0, kv * G + gq], wq[kv * G + gq], kv, kv * G + gq))
+    NU = 2 * len(streams)
+
+    with ExitStack() as ctx:
+        if MANUAL:
+            ctx.enter_context(tc.manual_schedule())
+        const = ctx.enter_context(tc.tile_pool(name="const", bufs=1))
+        qpool = ctx.enter_context(tc.tile_pool(name="qpool", bufs=6))
+        two = ctx.enter_context(tc.tile_pool(name="two", bufs=2))
+        three = ctx.enter_context(tc.tile_pool(name="three", bufs=3))
+        four = ctx.enter_context(tc.tile_pool(name="four", bufs=4))
+        psum = ctx.enter_context(tc.psum_pool(name="psum", bufs=2))
+
+        H = [dict() for n in range(NU)]
+        W = [dict() for s in range(len(streams))]
+        YK = []
+        for kv in range(HK):
+            ykc = const.tile([P, NB], U32, name="ykc%d" % kv, align_bytes=64)
+            yks = const.tile([P, NB], U8, name="yks%d" % kv, align_bytes=64)
+            YK.append((ykc, yks))
+
+        ident = const.tile([P, P], BF16)
+        perm = const.tile([P, P], BF16)
+        pool32 = const.tile([P, P // BS], F32)
+        poolm = const.tile([P, P // BS], BF16)
+        cs_raw = const.tile([P, 2, 4, HID], BF16)
+        cosT = const.tile([P, 4, NB], BF16)
+        sinT = const.tile([P, 4, NB], BF16)
+        mbias = const.tile([P, 4, NB], F32)
+        mw = const.tile([P, 4, NB, 2], I32)
+
+        def consts():
+            make_identity(nc, ident[:])
+            nc.vector.tensor_copy(
+                out=perm[:].rearrange("p (j b) -> p j b", j=BS),
+                in_=ident[:].rearrange("p (b j) -> p j b", j=BS),
+            )
+            nc.vector.tensor_reduce(
+                out=pool32[:], in_=ident[:].rearrange("p (b j) -> p b j", j=BS), axis=AX.X, op=ALU.add
+            )
+            nc.vector.tensor_scalar(out=poolm[:], in0=pool32[:], scalar1=1.0 / BS, scalar2=None, op0=ALU.mult)
+
+        def load_tables():
+            nc.sync.dma_start(out=cs_raw[:, 0], in_=cos[0].rearrange("(c p) h -> p c h", p=P))
+            nc.sync.dma_start(out=cs_raw[:, 1], in_=sin[0].rearrange("(c p) h -> p c h", p=P))
+
+        def load_mask():
+            mi = attention_mask.rearrange("a b i j -> (a b i) j").bitcast(I32)
+            assert mi.shape[1] == 2 * NB, "mask dtype %s" % str(attention_mask.dtype)
+            nc.sync.dma_start(out=mw[:].rearrange("p c j e -> p c (j e)"), in_=mi.rearrange("(c p) w -> p c w", p=P))
+
+        def tables():
+            for tb in range(2):
+                for m in range(4):
+                    tpt = T(psum, [P, NB], BF16, "tp")
+                    for c in range(4):
+                        nc.tensor.transpose(
+                            tpt[:, c * P:(c + 1) * P], cs_raw[:, tb, c, m * P:(m + 1) * P], ident[:]
+                        )
+                    if tb == 0:
+                        nc.scalar.copy(out=cosT[:, m, :], in_=tpt[:])
+                    elif m < 2:
+                        nc.scalar.mul(out=sinT[:, m, :], in_=tpt[:], mul=-1.0)
+                    else:
+                        nc.scalar.copy(out=sinT[:, m, :], in_=tpt[:])
+
+        def maskprep():
+            nc.vector.tensor_scalar(
+                out=mbias[:], in0=mw[:, :, :, 0], scalar1=-1.0, scalar2=1.0e9, op0=ALU.add, op1=ALU.mult
+            )
+
+        def T(pool, shape, dtype, tag, **kw):
+            return pool.tile(shape, dtype, tag=tag, name=tag, **kw)
+
+        def hs_of(n):
+            return slice((n % 2) * HB, (n % 2 + 1) * HB)
+
+        def load(n):
+            src = streams[n // 2][0].rearrange("(hh bh p) f -> hh p bh f", p=P, bh=16)
+            qt = T(qpool, [P, 16, D], BF16, "qt")
+            nc.sync.dma_start(out=qt[:], in_=src[n % 2])
+            H[n]["qt"] = qt
+
+        def load_w(s):
+            wr = T(three, [P, 4, HID], BF16, "wr")
+            nc.sync.dma_start(out=wr[:], in_=streams[s][1].rearrange("(t p) n -> p t n", p=P))
+            W[s]["wr"] = wr
+
+        def regroup(dst, src):
+            nc.scalar.copy(
+                out=dst.rearrange("p (c i) t -> p c t i", i=4), in_=src.rearrange("p t (c i) -> p c t i", i=4)
+            )
+
+        def quantise(grouped, codes, scales):
+            nc.vector.quantize_mx(
+                out=codes.bitcast(FP8X4), scales=scales, in_=grouped[:].rearrange("p n t -> p (n t)")
+            )
+
+        def rg_w(j):
+            wg = T(two, [P, HB, 4], BF16, "wg", align_bytes=64)
+            regroup(wg[:], W[j // 2]["wr"][:, :, hs_of(j)])
+            H[j]["wg"] = wg
+
+        def q_w(j):
+            s = j // 2
+            if j % 2 == 0:
+                W[s]["wc"] = T(two, [P, HID], U32, "wc", align_bytes=64)
+                W[s]["ws"] = T(two, [P, HID], U8, "ws", align_bytes=64)
+            quantise(H[j]["wg"], W[s]["wc"][:, hs_of(j)], W[s]["ws"][:, hs_of(j)])
+
+        def bank(n, b):
+            g, u = b // 2, b % 2
+            if b == 0:
+                H[n]["mean"] = T(psum, [P, 2, HB], F32, "mean")
+                H[n]["m1"] = T(two, [P, 2, 2, 4, P], BF16, "m1")
+            qt, mean = H[n]["qt"], H[n]["mean"]
+            tp = T(psum, [P, BS, 8, 16], BF16, "tp")
+            for b8 in range(8):
+                bh = g * 8 + b8
+                lhs = qt[:, bh, u * P:(u + 1) * P]
+                nc.tensor.transpose(tp[:, :, b8, :], lhs, perm[:].rearrange("p (j b) -> p j b", j=BS))
+                nc.tensor.matmul(mean[:, u, bh * 16:(bh + 1) * 16], lhsT=lhs, rhs=poolm[:], start=True, stop=True)
+            H[n]["tp%d" % b] = tp
+
+        def copy(n, b):
+            cp = T(three, [P, 4, P], BF16, "cp")
+            nc.scalar.copy(out=cp[:], in_=H[n]["tp%d" % b][:, 4:8].rearrange("p j b l -> p j (b l)"))
+            H[n]["cp%d" % b] = cp
+
+        def lev1(n, b):
+            nc.vector.tensor_tensor(
+                out=H[n]["m1"][:, b % 2, b // 2], in0=H[n]["tp%d" % b][:, 0:4].rearrange("p j b l -> p j (b l)"),
+                in1=H[n]["cp%d" % b][:], op=ALU.max,
+            )
+
+        def lev23(n):
+            m1 = H[n]["m1"]
+            mx2 = T(two, [P, 2, 2, 2, P], BF16, "mx2")
+            nc.vector.tensor_tensor(out=mx2[:], in0=m1[:, :, :, 0:2, :], in1=m1[:, :, :, 2:4, :], op=ALU.max)
+            z = T(three, [P, 4, HB], BF16, "z")
+            nc.vector.tensor_tensor(
+                out=z[:, 2:4, :].rearrange("p u (g w) -> p u g w", g=2),
+                in0=mx2[:, :, :, 0, :], in1=mx2[:, :, :, 1, :], op=ALU.max,
+            )
+            H[n]["z"] = z
+
+        def mevac(n):
+            nc.scalar.copy(out=H[n]["z"][:, 0:2, :], in_=H[n]["mean"][:])
+
+        def rg_z(n):
+            pg = T(two, [P, HB, 4], BF16, "pg", align_bytes=64)
+            regroup(pg[:], H[n]["z"][:])
+            H[n]["pg"] = pg
+
+        def q_p(n):
+            H[n]["pc"] = T(two, [P, HB], U32, "pc", align_bytes=64)
+            H[n]["ps"] = T(two, [P, HB], U8, "ps", align_bytes=64)
+            quantise(H[n]["pg"], H[n]["pc"][:], H[n]["ps"][:])
+
+        def mx(n):
+            wc, ws = W[n // 2]["wc"], W[n // 2]["ws"]
+            H[n]["x0"] = T(psum, [P, 2, HB], F32, "x")
+            H[n]["x1"] = T(psum, [P, 2, HB], F32, "x")
+            for m in range(4):
+                nc.tensor.matmul_mx(
+                    out=H[n]["x%d" % (m // 2)][:, m % 2, :],
+                    lhsT=wc[:, m * P:(m + 1) * P].bitcast(FP8X4), lhsT_scale=ws[:, m * P:(m + 1) * P],
+                    rhs=H[n]["pc"][:].bitcast(FP8X4), rhs_scale=H[n]["ps"][:], start=True, stop=True,
+                )
+
+        def mult(n, i):
+            if i == 0:
+                H[n]["ta"] = T(three, [P, 4, HB], F32, "ta")
+                H[n]["tb"] = T(three, [P, 4, HB], F32, "tb")
+            x = H[n]["x%d" % (i // 2)]
+            own = slice(2 * (i // 2), 2 * (i // 2) + 2)
+            other = slice(2 - 2 * (i // 2), 4 - 2 * (i // 2))
+            if i % 2 == 0:
+                nc.vector.tensor_tensor(out=H[n]["ta"][:, own], in0=x[:], in1=cosT[:, own, hs_of(n)], op=ALU.mult)
+            else:
+                nc.vector.tensor_tensor(out=H[n]["tb"][:, other], in0=x[:], in1=sinT[:, other, hs_of(n)], op=ALU.mult)
+
+        def add(n):
+            yg = T(three, [P, HB, 4], BF16, "yg", align_bytes=64)
+            eng = nc.gpsimd if ADD_ON_G else nc.vector
+            eng.tensor_tensor(
+                out=yg[:], in0=H[n]["ta"][:].rearrange("p m w -> p w m"),
+                in1=H[n]["tb"][:].rearrange("p m w -> p w m"), op=ALU.add,
+            )
+            H[n]["yg"] = yg
+
+        def q_y(n):
+            kv, h = streams[n // 2][2], streams[n // 2][3]
+            if h is None:
+                quantise(H[n]["yg"], YK[kv][0][:, hs_of(n)], YK[kv][1][:, hs_of(n)])
+            else:
+                H[n]["yc"] = T(three, [P, HB], U32, "yc", align_bytes=64)
+                H[n]["ys"] = T(three, [P, HB], U8, "ys", align_bytes=64)
+                quantise(H[n]["yg"], H[n]["yc"][:], H[n]["ys"][:])
+
+        def score(n, cc):
+            kv = streams[n // 2][2]
+            sc = T(psum, [P, NB], F32, "sc")
+            nc.tensor.matmul_mx(
+                out=sc[:],
+                lhsT=H[n]["yc"][:, cc * P:(cc + 1) * P].bitcast(FP8X4), lhsT_scale=H[n]["ys"][:, cc * P:(cc + 1) * P],
+                rhs=YK[kv][0][:].bitcast(FP8X4), rhs_scale=YK[kv][1][:], start=True, stop=True,
+            )
+            H[n]["sc%d" % cc] = sc
+
+        def stt(n, cc):
+            if cc == 0:
+                H[n]["t2"] = T(four, [P, 2, NB], F32, "t2")
+            nc.vector.scalar_tensor_tensor(
+                out=H[n]["t2"][:, cc, :], in0=H[n]["sc%d" % cc][:], scalar=SCALE,
+                in1=mbias[:, 2 * (n % 2) + cc, :], op0=ALU.mult, op1=ALU.add,
+            )
+
+        def red(n):
+            H[n]["nmx"] = T(four, [P, 2], F32, "nmx")
+            nc.vector.tensor_reduce(out=H[n]["nmx"][:], in_=H[n]["t2"][:], axis=AX.X, op=ALU.max, negate=True)
+
+        def expo(n, cc):
+            if cc == 0:
+                H[n]["ssum"] = T(four, [P, 2], F32, "ssum")
+            nc.scalar.activation(
+                out=H[n]["t2"][:, cc, :], in_=H[n]["t2"][:, cc, :], func=ACT.Exp,
+                bias=H[n]["nmx"][:, cc:cc + 1], scale=1.0, accum_out=H[n]["ssum"][:, cc:cc + 1],
+            )
+
+        def rec(n):
+            H[n]["rs"] = T(four, [P, 2], F32, "rs")
+            nc.vector.reciprocal(out=H[n]["rs"][:], in_=H[n]["ssum"][:])
+
+        def norm(n, cc):
+            nc.scalar.activation(
+                out=H[n]["t2"][:, cc, :], in_=H[n]["t2"][:, cc, :], func=ACT.Copy, scale=H[n]["rs"][:, cc:cc + 1]
+            )
+
+        def store(n):
+            h = streams[n // 2][3]
+            nc.scalar.dma_start(
+                out=out[0, h, hs_of(n), :].rearrange("(c p) j -> p c j", p=P), in_=H[n]["t2"][:]
+            )
+
+        def ok(n):
+            return 0 <= n < NU
+
+        def isq(n):
+            return ok(n) and streams[n // 2][3] is not None
+
+        consts()
+        load(0)
+        load_w(0)
+        load(1)
+        load_tables()
+        load_w(1)
+        load(2)
+        load(3)
+        load_mask()
+        load(4)
+        for t in range(NU + 5):
+            if ok(t + 5):
+                load(t + 5)
+            if t % 2 == 0 and t // 2 + 2 < len(streams):
+                load_w(t // 2 + 2)
+            if ok(t - 1):
+                rg_z(t - 1)
+            if t == 1:
+                q_w(0)
+            if ok(t) and t >= 1:
+                q_w(t)
+            if ok(t - 3):
+                q_y(t - 3)
+            for b in range(4):
+                if ok(t):
+                    bank(t, b)
+                    copy(t, b)
+                if ok(t - 2):
+                    mult(t - 2, b)
+                if ok(t):
+                    lev1(t, b)
+                if b < 2 and isq(t - 4):
+                    expo(t - 4, b)
+                if b == 1 and isq(t - 3):
+                    score(t - 3, 0)
+                    score(t - 3, 1)
+            if ok(t - 2):
+                add(t - 2)
+            if isq(t - 3):
+                stt(t - 3, 0)
+                stt(t - 3, 1)
+                red(t - 3)
+            if ok(t - 1):
+                q_p(t - 1)
+                mx(t - 1)
+            if ok(t):
+                lev23(t)
+                mevac(t)
+            if isq(t - 4):
+                rec(t - 4)
+            if t == 0:
+                rg_w(0)
+            if ok(t + 1):
+                rg_w(t + 1)
+            if isq(t - 4):
+                norm(t - 4, 0)
+                norm(t - 4, 1)
+                store(t - 4)
+            if t == 0:
+                tables()
+            if t == 3:
+                maskprep()

@@ -22,7 +22,7 @@ HB = NB // 2
 FLOPS = 2 * NB * (2 * D) * HID * (HQ + HK) + 2 * NB * NB * HID * HQ
 SCALE = 1.0 / math.sqrt(HID)
 MANUAL = False
-ADD_ON_G = True
+ADD_ON_G = False
 
 
 def tile_attngate_kernel(tc, q, k, attention_mask, cos, sin, wq, wk, out):

@@ -43,6 +43,7 @@ def tile_attngate_kernel(tc, q, k, attention_mask, cos, sin, wq, wk, out):
         three = ctx.enter_context(tc.tile_pool(name="three", bufs=3))
         four = ctx.enter_context(tc.tile_pool(name="four", bufs=4))
         psum = ctx.enter_context(tc.psum_pool(name="psum", bufs=2))
+        psum1 = ctx.enter_context(tc.psum_pool(name="psum1", bufs=1))
 
         H = [dict() for n in range(NU)]
         W = [dict() for s in range(len(streams))]
@@ -57,13 +58,14 @@ def tile_attngate_kernel(tc, q, k, attention_mask, cos, sin, wq, wk, out):
         pool32 = const.tile([P, P // BS], F32)
         poolm = const.tile([P, P // BS], BF16)
         cs_raw = const.tile([P, 2, 4, HID], BF16)
-        cosT = const.tile([P, 4, NB], BF16)
-        sinT = const.tile([P, 4, NB], BF16)
+        sinS = const.tile([P, 4, HID], BF16)
+        identf = const.tile([P, P], F32)
         mbias = const.tile([P, 4, NB], F32)
         mw = const.tile([P, 4, NB, 2], I32)
 
         def consts():
             make_identity(nc, ident[:])
+            make_identity(nc, identf[:])
             nc.vector.tensor_copy(
                 out=perm[:].rearrange("p (j b) -> p j b", j=BS),
                 in_=ident[:].rearrange("p (b j) -> p j b", j=BS),
@@ -83,19 +85,8 @@ def tile_attngate_kernel(tc, q, k, attention_mask, cos, sin, wq, wk, out):
             nc.sync.dma_start(out=mw[:].rearrange("p c j e -> p c (j e)"), in_=mi.rearrange("(c p) w -> p c w", p=P))
 
         def tables():
-            for tb in range(2):
-                for m in range(4):
-                    tpt = T(psum, [P, NB], BF16, "tp")
-                    for c in range(4):
-                        nc.tensor.transpose(
-                            tpt[:, c * P:(c + 1) * P], cs_raw[:, tb, c, m * P:(m + 1) * P], ident[:]
-                        )
-                    if tb == 0:
-                        nc.scalar.copy(out=cosT[:, m, :], in_=tpt[:])
-                    elif m < 2:
-                        nc.scalar.mul(out=sinT[:, m, :], in_=tpt[:], mul=-1.0)
-                    else:
-                        nc.scalar.copy(out=sinT[:, m, :], in_=tpt[:])
+            nc.scalar.mul(out=sinS[:, :, 0:D], in_=cs_raw[:, 1, :, 0:D], mul=-1.0)
+            nc.scalar.copy(out=sinS[:, :, D:HID], in_=cs_raw[:, 1, :, D:HID])
 
         def maskprep():
             nc.vector.tensor_scalar(
@@ -144,7 +135,7 @@ def tile_attngate_kernel(tc, q, k, attention_mask, cos, sin, wq, wk, out):
         def bank(n, b):
             g, u = b // 2, b % 2
             if b == 0:
-                H[n]["mean"] = T(psum, [P, 2, HB], F32, "mean")
+                H[n]["mean"] = T(psum1, [P, 2, HB], F32, "mean")
                 H[n]["m1"] = T(two, [P, 2, 2, 4, P], BF16, "m1")
             qt, mean = H[n]["qt"], H[n]["mean"]
             tp = T(psum, [P, BS, 8, 16], BF16, "tp")
@@ -192,35 +183,40 @@ def tile_attngate_kernel(tc, q, k, attention_mask, cos, sin, wq, wk, out):
 
         def mx(n):
             wc, ws = W[n // 2]["wc"], W[n // 2]["ws"]
-            H[n]["x0"] = T(psum, [P, 2, HB], F32, "x")
-            H[n]["x1"] = T(psum, [P, 2, HB], F32, "x")
-            for m in range(4):
+            for cc in range(2):
+                x = T(psum, [P, HID], F32, "x")
                 nc.tensor.matmul_mx(
-                    out=H[n]["x%d" % (m // 2)][:, m % 2, :],
-                    lhsT=wc[:, m * P:(m + 1) * P].bitcast(FP8X4), lhsT_scale=ws[:, m * P:(m + 1) * P],
-                    rhs=H[n]["pc"][:].bitcast(FP8X4), rhs_scale=H[n]["ps"][:], start=True, stop=True,
+                    out=x[:],
+                    lhsT=H[n]["pc"][:, cc * P:(cc + 1) * P].bitcast(FP8X4), lhsT_scale=H[n]["ps"][:, cc * P:(cc + 1) * P],
+                    rhs=wc[:].bitcast(FP8X4), rhs_scale=ws[:], start=True, stop=True,
                 )
+                H[n]["x%d" % cc] = x
 
         def mult(n, i):
+            cc = i // 2
+            c = 2 * (n % 2) + cc
+            x = H[n]["x%d" % cc]
             if i == 0:
-                H[n]["ta"] = T(three, [P, 4, HB], F32, "ta")
-                H[n]["tb"] = T(three, [P, 4, HB], F32, "tb")
-            x = H[n]["x%d" % (i // 2)]
-            own = slice(2 * (i // 2), 2 * (i // 2) + 2)
-            other = slice(2 - 2 * (i // 2), 4 - 2 * (i // 2))
+                H[n]["yg"] = T(three, [P, HB, 4], BF16, "yg", align_bytes=64)
             if i % 2 == 0:
-                nc.vector.tensor_tensor(out=H[n]["ta"][:, own], in0=x[:], in1=cosT[:, own, hs_of(n)], op=ALU.mult)
+                ta = T(three, [P, HID], F32, "ta")
+                nc.vector.tensor_tensor(out=ta[:], in0=x[:], in1=cs_raw[:, 0, c, :], op=ALU.mult)
+                H[n]["ta"] = ta
             else:
-                nc.vector.tensor_tensor(out=H[n]["tb"][:, other], in0=x[:], in1=sinT[:, other, hs_of(n)], op=ALU.mult)
+                ta = H[n]["ta"]
+                tb = T(three, [P, HID], F32, "tb")
+                nc.vector.tensor_tensor(out=tb[:, 0:D], in0=x[:, D:HID], in1=sinS[:, c, 0:D], op=ALU.mult)
+                nc.vector.tensor_tensor(out=tb[:, D:HID], in0=x[:, 0:D], in1=sinS[:, c, D:HID], op=ALU.mult)
+                yt = T(psum, [P, 4, P], F32, "yt")
+                for m in range(4):
+                    nc.tensor.matmul(yt[:, m, :], lhsT=ta[:, m * P:(m + 1) * P], rhs=identf[:], is_transpose=True,
+                                     start=True, stop=False)
+                    nc.tensor.matmul(yt[:, m, :], lhsT=tb[:, m * P:(m + 1) * P], rhs=identf[:], is_transpose=True,
+                                     start=False, stop=True)
+                nc.scalar.copy(out=H[n]["yg"][:, cc * P:(cc + 1) * P, :], in_=yt[:].rearrange("p m b -> p b m"))
 
         def add(n):
-            yg = T(three, [P, HB, 4], BF16, "yg", align_bytes=64)
-            eng = nc.gpsimd if ADD_ON_G else nc.vector
-            eng.tensor_tensor(
-                out=yg[:], in0=H[n]["ta"][:].rearrange("p m w -> p w m"),
-                in1=H[n]["tb"][:].rearrange("p m w -> p w m"), op=ALU.add,
-            )
-            H[n]["yg"] = yg
+            return None
 
         def q_y(n):
             kv, h = streams[n // 2][2], streams[n // 2][3]
@@ -233,7 +229,7 @@ def tile_attngate_kernel(tc, q, k, attention_mask, cos, sin, wq, wk, out):
 
         def score(n, cc):
             kv = streams[n // 2][2]
-            sc = T(psum, [P, NB], F32, "sc")
+            sc = T(psum1, [P, NB], F32, "sc")
             nc.tensor.matmul_mx(
                 out=sc[:],
                 lhsT=H[n]["yc"][:, cc * P:(cc + 1) * P].bitcast(FP8X4), lhsT_scale=H[n]["ys"][:, cc * P:(cc + 1) * P],

@@ -38,7 +38,7 @@ def tile_attngate_kernel(tc, q, k, attention_mask, cos, sin, wq, wk, out):
         if MANUAL:
             ctx.enter_context(tc.manual_schedule())
         const = ctx.enter_context(tc.tile_pool(name="const", bufs=1))
-        qpool = ctx.enter_context(tc.tile_pool(name="qpool", bufs=6))
+        qpool = ctx.enter_context(tc.tile_pool(name="qpool", bufs=5))
         two = ctx.enter_context(tc.tile_pool(name="two", bufs=2))
         three = ctx.enter_context(tc.tile_pool(name="three", bufs=3))
         four = ctx.enter_context(tc.tile_pool(name="four", bufs=4))
@@ -54,7 +54,6 @@ def tile_attngate_kernel(tc, q, k, attention_mask, cos, sin, wq, wk, out):
             YK.append((ykc, yks))
 
         ident = const.tile([P, P], BF16)
-        perm = const.tile([P, P], BF16)
         pool32 = const.tile([P, P // BS], F32)
         poolm = const.tile([P, P // BS], BF16)
         cs_raw = const.tile([P, 2, 4, HID], BF16)
@@ -66,10 +65,6 @@ def tile_attngate_kernel(tc, q, k, attention_mask, cos, sin, wq, wk, out):
         def consts():
             make_identity(nc, ident[:])
             make_identity(nc, identf[:])
-            nc.vector.tensor_copy(
-                out=perm[:].rearrange("p (j b) -> p j b", j=BS),
-                in_=ident[:].rearrange("p (b j) -> p j b", j=BS),
-            )
             nc.vector.tensor_reduce(
                 out=pool32[:], in_=ident[:].rearrange("p (b j) -> p b j", j=BS), axis=AX.X, op=ALU.add
             )
@@ -100,10 +95,16 @@ def tile_attngate_kernel(tc, q, k, attention_mask, cos, sin, wq, wk, out):
             return slice((n % 2) * HB, (n % 2 + 1) * HB)
 
         def load(n):
-            src = streams[n // 2][0].rearrange("(hh bh p) f -> hh p bh f", p=P, bh=16)
-            qt = T(qpool, [P, 16, D], BF16, "qt")
-            nc.sync.dma_start(out=qt[:], in_=src[n % 2])
-            H[n]["qt"] = qt
+            x = streams[n // 2][0]
+            qa = T(qpool, [P, 2, BS, D], BF16, "qa")
+            nc.sync.dma_start(
+                out=qa[:].rearrange("p c j f -> p c (j f)"),
+                in_=x.rearrange("(hh c p j) f -> hh p c (j f)", c=2, p=P, j=BS)[n % 2],
+            )
+            qp = T(qpool, [P, 16, D], BF16, "qp")
+            nc.sync.dma_start(out=qp[:], in_=x.rearrange("(hh bh p) f -> hh p bh f", p=P, bh=16)[n % 2])
+            H[n]["qa"] = qa
+            H[n]["qp"] = qp
 
         def load_w(s):
             wr = T(three, [P, 4, HID], BF16, "wr")
@@ -133,39 +134,43 @@ def tile_attngate_kernel(tc, q, k, attention_mask, cos, sin, wq, wk, out):
             quantise(H[j]["wg"], W[s]["wc"][:, hs_of(j)], W[s]["ws"][:, hs_of(j)])
 
         def bank(n, b):
-            g, u = b // 2, b % 2
             if b == 0:
-                H[n]["mean"] = T(psum1, [P, 2, HB], F32, "mean")
-                H[n]["m1"] = T(two, [P, 2, 2, 4, P], BF16, "m1")
-            qt, mean = H[n]["qt"], H[n]["mean"]
-            tp = T(psum, [P, BS, 8, 16], BF16, "tp")
-            for b8 in range(8):
-                bh = g * 8 + b8
-                lhs = qt[:, bh, u * P:(u + 1) * P]
-                nc.tensor.transpose(tp[:, :, b8, :], lhs, perm[:].rearrange("p (j b) -> p j b", j=BS))
-                nc.tensor.matmul(mean[:, u, bh * 16:(bh + 1) * 16], lhsT=lhs, rhs=poolm[:], start=True, stop=True)
-            H[n]["tp%d" % b] = tp
+                mean = T(psum, [P, 2, HB], F32, "mean")
+                H[n]["mean"] = mean
+                for u in range(2):
+                    for bh in range(16):
+                        nc.tensor.matmul(
+                            mean[:, u, bh * 16:(bh + 1) * 16], lhsT=H[n]["qp"][:, bh, u * P:(u + 1) * P],
+                            rhs=poolm[:], start=True, stop=True,
+                        )
 
         def copy(n, b):
-            cp = T(three, [P, 4, P], BF16, "cp")
-            nc.scalar.copy(out=cp[:], in_=H[n]["tp%d" % b][:, 4:8].rearrange("p j b l -> p j (b l)"))
-            H[n]["cp%d" % b] = cp
+            return None
 
         def lev1(n, b):
-            nc.vector.tensor_tensor(
-                out=H[n]["m1"][:, b % 2, b // 2], in0=H[n]["tp%d" % b][:, 0:4].rearrange("p j b l -> p j (b l)"),
-                in1=H[n]["cp%d" % b][:], op=ALU.max,
-            )
+            qa = H[n]["qa"]
+            if b == 0:
+                m1 = T(two, [P, 2, 4, D], BF16, "m1")
+                nc.vector.tensor_tensor(out=m1[:], in0=qa[:, :, 0:4, :], in1=qa[:, :, 4:8, :], op=ALU.max)
+                H[n]["m1"] = m1
+            elif b == 1:
+                m1 = H[n]["m1"]
+                m2 = T(two, [P, 2, 2, D], BF16, "mx2")
+                nc.vector.tensor_tensor(out=m2[:], in0=m1[:, :, 0:2, :], in1=m1[:, :, 2:4, :], op=ALU.max)
+                H[n]["m2"] = m2
+            elif b == 2:
+                m2 = H[n]["m2"]
+                m3 = T(two, [P, 2, D], BF16, "m3")
+                nc.vector.tensor_tensor(out=m3[:], in0=m2[:, :, 0, :], in1=m2[:, :, 1, :], op=ALU.max)
+                mt = T(psum1, [P, 2, HB], BF16, "mt")
+                for c in range(2):
+                    for u in range(2):
+                        nc.tensor.transpose(mt[:, u, c * P:(c + 1) * P], m3[:, c, u * P:(u + 1) * P], ident[:])
+                H[n]["mt"] = mt
 
         def lev23(n):
-            m1 = H[n]["m1"]
-            mx2 = T(two, [P, 2, 2, 2, P], BF16, "mx2")
-            nc.vector.tensor_tensor(out=mx2[:], in0=m1[:, :, :, 0:2, :], in1=m1[:, :, :, 2:4, :], op=ALU.max)
             z = T(three, [P, 4, HB], BF16, "z")
-            nc.vector.tensor_tensor(
-                out=z[:, 2:4, :].rearrange("p u (g w) -> p u g w", g=2),
-                in0=mx2[:, :, :, 0, :], in1=mx2[:, :, :, 1, :], op=ALU.max,
-            )
+            nc.scalar.copy(out=z[:, 2:4, :], in_=H[n]["mt"][:])
             H[n]["z"] = z
 
         def mevac(n):
@@ -285,12 +290,11 @@ def tile_attngate_kernel(tc, q, k, attention_mask, cos, sin, wq, wk, out):
         load_tables()
         load_w(1)
         load(2)
-        load(3)
         load_mask()
-        load(4)
+        load(3)
         for t in range(NU + 5):
-            if ok(t + 5):
-                load(t + 5)
+            if ok(t + 4):
+                load(t + 4)
             if t % 2 == 0 and t // 2 + 2 < len(streams):
                 load_w(t // 2 + 2)
             if ok(t - 1):

@@ -56,8 +56,8 @@ def tile_attngate_kernel(tc, q, k, attention_mask, cos, sin, wq, wk, out):
         ident = const.tile([P, P], BF16)
         pool32 = const.tile([P, P // BS], F32)
         poolm = const.tile([P, P // BS], BF16)
-        cs_raw = const.tile([P, 2, 4, HID], BF16)
-        sinS = const.tile([P, 4, HID], BF16)
+        cs = const.tile([P, 4, 2, HID], BF16)
+        sraw = const.tile([P, 4, HID], BF16)
         identf = const.tile([P, P], F32)
         mbias = const.tile([P, 4, NB], F32)
         mw = const.tile([P, 4, NB, 2], I32)
@@ -71,8 +71,8 @@ def tile_attngate_kernel(tc, q, k, attention_mask, cos, sin, wq, wk, out):
             nc.vector.tensor_scalar(out=poolm[:], in0=pool32[:], scalar1=1.0 / BS, scalar2=None, op0=ALU.mult)
 
         def load_tables():
-            nc.sync.dma_start(out=cs_raw[:, 0], in_=cos[0].rearrange("(c p) h -> p c h", p=P))
-            nc.sync.dma_start(out=cs_raw[:, 1], in_=sin[0].rearrange("(c p) h -> p c h", p=P))
+            nc.sync.dma_start(out=cs[:, :, 0, :], in_=cos[0].rearrange("(c p) h -> p c h", p=P))
+            nc.sync.dma_start(out=sraw[:], in_=sin[0].rearrange("(c p) h -> p c h", p=P))
 
         def load_mask():
             mi = attention_mask.rearrange("a b i j -> (a b i) j").bitcast(I32)
@@ -80,8 +80,8 @@ def tile_attngate_kernel(tc, q, k, attention_mask, cos, sin, wq, wk, out):
             nc.sync.dma_start(out=mw[:].rearrange("p c j e -> p c (j e)"), in_=mi.rearrange("(c p) w -> p c w", p=P))
 
         def tables():
-            nc.scalar.mul(out=sinS[:, :, 0:D], in_=cs_raw[:, 1, :, 0:D], mul=-1.0)
-            nc.scalar.copy(out=sinS[:, :, D:HID], in_=cs_raw[:, 1, :, D:HID])
+            nc.scalar.copy(out=cs[:, :, 1, 0:D], in_=sraw[:, :, D:HID])
+            nc.scalar.mul(out=cs[:, :, 1, D:HID], in_=sraw[:, :, 0:D], mul=-1.0)
 
         def maskprep():
             nc.vector.tensor_scalar(
@@ -122,16 +122,17 @@ def tile_attngate_kernel(tc, q, k, attention_mask, cos, sin, wq, wk, out):
             )
 
         def rg_w(j):
-            wg = T(two, [P, HB, 4], BF16, "wg", align_bytes=64)
-            regroup(wg[:], W[j // 2]["wr"][:, :, hs_of(j)])
-            H[j]["wg"] = wg
+            s = j // 2
+            if j % 2 == 0:
+                W[s]["wg"] = T(two, [P, HID, 4], BF16, "wg", align_bytes=64)
+            regroup(W[s]["wg"][:, hs_of(j), :], W[s]["wr"][:, :, hs_of(j)])
 
         def q_w(j):
             s = j // 2
-            if j % 2 == 0:
+            if j % 2 == 1:
                 W[s]["wc"] = T(two, [P, HID], U32, "wc", align_bytes=64)
                 W[s]["ws"] = T(two, [P, HID], U8, "ws", align_bytes=64)
-            quantise(H[j]["wg"], W[s]["wc"][:, hs_of(j)], W[s]["ws"][:, hs_of(j)])
+                quantise(W[s]["wg"], W[s]["wc"][:], W[s]["ws"][:])
 
         def bank(n, b):
             if b == 0:
@@ -198,27 +199,24 @@ def tile_attngate_kernel(tc, q, k, attention_mask, cos, sin, wq, wk, out):
                 H[n]["x%d" % cc] = x
 
         def mult(n, i):
+            if i % 2 == 1:
+                return None
             cc = i // 2
-            c = 2 * (n % 2) + cc
             x = H[n]["x%d" % cc]
             if i == 0:
                 H[n]["yg"] = T(three, [P, HB, 4], BF16, "yg", align_bytes=64)
-            if i % 2 == 0:
-                ta = T(three, [P, HID], F32, "ta")
-                nc.vector.tensor_tensor(out=ta[:], in0=x[:], in1=cs_raw[:, 0, c, :], op=ALU.mult)
-                H[n]["ta"] = ta
-            else:
-                ta = H[n]["ta"]
-                tb = T(three, [P, HID], F32, "tb")
-                nc.vector.tensor_tensor(out=tb[:, 0:D], in0=x[:, D:HID], in1=sinS[:, c, 0:D], op=ALU.mult)
-                nc.vector.tensor_tensor(out=tb[:, D:HID], in0=x[:, 0:D], in1=sinS[:, c, D:HID], op=ALU.mult)
-                yt = T(psum, [P, 4, P], F32, "yt")
-                for m in range(4):
-                    nc.tensor.matmul(yt[:, m, :], lhsT=ta[:, m * P:(m + 1) * P], rhs=identf[:], is_transpose=True,
-                                     start=True, stop=False)
-                    nc.tensor.matmul(yt[:, m, :], lhsT=tb[:, m * P:(m + 1) * P], rhs=identf[:], is_transpose=True,
-                                     start=False, stop=True)
-                nc.scalar.copy(out=H[n]["yg"][:, cc * P:(cc + 1) * P, :], in_=yt[:].rearrange("p m b -> p b m"))
+            ab = T(three, [P, 2, HID], F32, "ab")
+            nc.vector.tensor_tensor(
+                out=ab[:], in0=x[:].unsqueeze(1).to_broadcast([P, 2, HID]), in1=cs[:, 2 * (n % 2) + cc], op=ALU.mult
+            )
+            yt = T(psum, [P, 4, P], F32, "yt")
+            for m in range(4):
+                mo = (m + 2) % 4
+                nc.tensor.matmul(yt[:, m, :], lhsT=ab[:, 0, m * P:(m + 1) * P], rhs=identf[:], is_transpose=True,
+                                 start=True, stop=False)
+                nc.tensor.matmul(yt[:, m, :], lhsT=ab[:, 1, mo * P:(mo + 1) * P], rhs=identf[:], is_transpose=True,
+                                 start=False, stop=True)
+            nc.scalar.copy(out=H[n]["yg"][:, cc * P:(cc + 1) * P, :], in_=yt[:].rearrange("p m b -> p b m"))
 
         def add(n):
             return None

@@ -108,7 +108,10 @@ def tile_attngate_kernel(tc, q, k, attention_mask, cos, sin, wq, wk, out):
 
         def load_w(s):
             wr = T(three, [P, 4, HID], BF16, "wr")
-            nc.sync.dma_start(out=wr[:], in_=streams[s][1].rearrange("(t p) n -> p t n", p=P))
+            nc.sync.dma_start(
+                out=wr[:].rearrange("p (u e) n -> p u (e n)", u=2),
+                in_=streams[s][1].rearrange("(u p e) n -> p u (e n)", u=2, p=P),
+            )
             W[s]["wr"] = wr
 
         def regroup(dst, src):
@@ -141,7 +144,7 @@ def tile_attngate_kernel(tc, q, k, attention_mask, cos, sin, wq, wk, out):
                 for u in range(2):
                     for bh in range(16):
                         nc.tensor.matmul(
-                            mean[:, u, bh * 16:(bh + 1) * 16], lhsT=H[n]["qp"][:, bh, u * P:(u + 1) * P],
+                            mean[:, u, bh * 16:(bh + 1) * 16], lhsT=H[n]["qp"][:, bh, u::2],
                             rhs=poolm[:], start=True, stop=True,
                         )
 
@@ -163,23 +166,29 @@ def tile_attngate_kernel(tc, q, k, attention_mask, cos, sin, wq, wk, out):
                 m2 = H[n]["m2"]
                 m3 = T(two, [P, 2, D], BF16, "m3")
                 nc.vector.tensor_tensor(out=m3[:], in0=m2[:, :, 0, :], in1=m2[:, :, 1, :], op=ALU.max)
-                mt = T(psum1, [P, 2, HB], BF16, "mt")
+                mt = T(psum1, [P, 2, P], F32, "mt")
                 for c in range(2):
-                    for u in range(2):
-                        nc.tensor.transpose(mt[:, u, c * P:(c + 1) * P], m3[:, c, u * P:(u + 1) * P], ident[:])
+                    nc.tensor.matmul(mt[:, c, :], lhsT=m3[:, c, :].bitcast(F32), rhs=identf[:], is_transpose=True,
+                                     start=True, stop=True)
                 H[n]["mt"] = mt
 
         def lev23(n):
-            z = T(three, [P, 4, HB], BF16, "z")
-            nc.scalar.copy(out=z[:, 2:4, :], in_=H[n]["mt"][:])
+            z = T(three, [P, 2, HB], F32, "z")
+            nc.scalar.copy(out=z[:, 1, :], in_=H[n]["mt"][:].rearrange("p c b -> p (c b)"))
             H[n]["z"] = z
 
         def mevac(n):
-            nc.scalar.copy(out=H[n]["z"][:, 0:2, :], in_=H[n]["mean"][:])
+            nc.scalar.copy(
+                out=H[n]["z"][:, 0, :].bitcast(BF16).rearrange("p (b e) -> p b e", e=2),
+                in_=H[n]["mean"][:].rearrange("p e b -> p b e"),
+            )
 
         def rg_z(n):
             pg = T(two, [P, HB, 4], BF16, "pg", align_bytes=64)
-            regroup(pg[:], H[n]["z"][:])
+            nc.scalar.copy(
+                out=pg[:].rearrange("p b t -> p (b t)").bitcast(F32).rearrange("p (b s) -> p b s", s=2),
+                in_=H[n]["z"][:].rearrange("p s b -> p b s"),
+            )
             H[n]["pg"] = pg
 
         def q_p(n):

@@ -22,6 +22,7 @@ HB = NB // 2
 FLOPS = 2 * NB * (2 * D) * HID * (HQ + HK) + 2 * NB * NB * HID * HQ
 SCALE = 1.0 / math.sqrt(HID)
 MANUAL = False
+PAIRED = (1, 3)
 ADD_ON_G = False
 
 
@@ -56,6 +57,9 @@ def tile_attngate_kernel(tc, q, k, attention_mask, cos, sin, wq, wk, out):
         ident = const.tile([P, P], BF16)
         pool32 = const.tile([P, P // BS], F32)
         poolm = const.tile([P, P // BS], BF16)
+        pool32b = const.tile([P, P // 4], F32)
+        poolm2 = const.tile([P, P // 4], BF16)
+        permp = const.tile([P, P], F32)
         cs = const.tile([P, 4, 2, HID], BF16)
         sraw = const.tile([P, 4, HID], BF16)
         identf = const.tile([P, P], F32)
@@ -69,6 +73,13 @@ def tile_attngate_kernel(tc, q, k, attention_mask, cos, sin, wq, wk, out):
                 out=pool32[:], in_=ident[:].rearrange("p (b j) -> p b j", j=BS), axis=AX.X, op=ALU.add
             )
             nc.vector.tensor_scalar(out=poolm[:], in0=pool32[:], scalar1=1.0 / BS, scalar2=None, op0=ALU.mult)
+            nc.vector.tensor_reduce(
+                out=pool32b[:], in_=ident[:].rearrange("p (b j) -> p b j", j=4), axis=AX.X, op=ALU.add
+            )
+            nc.vector.tensor_scalar(out=poolm2[:], in0=pool32b[:], scalar1=1.0 / BS, scalar2=None, op0=ALU.mult)
+            nc.vector.tensor_copy(
+                out=permp[:].rearrange("p (j b) -> p j b", j=4), in_=identf[:].rearrange("p (b j) -> p j b", j=4)
+            )
 
         def load_tables():
             nc.sync.dma_start(out=cs[:, :, 0, :], in_=cos[0].rearrange("(c p) h -> p c h", p=P))
@@ -94,8 +105,19 @@ def tile_attngate_kernel(tc, q, k, attention_mask, cos, sin, wq, wk, out):
         def hs_of(n):
             return slice((n % 2) * HB, (n % 2 + 1) * HB)
 
+        def paired(n):
+            return (n // 2) % 5 in PAIRED
+
         def load(n):
             x = streams[n // 2][0]
+            if paired(n):
+                q2 = T(qpool, [P, 8, 2, D], BF16, "qp")
+                nc.sync.dma_start(
+                    out=q2[:].rearrange("p g e f -> p g (e f)"),
+                    in_=x.rearrange("(hh g p e) f -> hh p g (e f)", g=8, p=P, e=2)[n % 2],
+                )
+                H[n]["q2"] = q2
+                return
             qa = T(qpool, [P, 2, BS, D], BF16, "qa")
             nc.sync.dma_start(
                 out=qa[:].rearrange("p c j f -> p c (j f)"),
@@ -139,8 +161,17 @@ def tile_attngate_kernel(tc, q, k, attention_mask, cos, sin, wq, wk, out):
 
         def bank(n, b):
             if b == 0:
-                mean = T(psum, [P, 2, HB], F32, "mean")
+                mean = T(psum1, [P, 2, HB], F32, "mean")
                 H[n]["mean"] = mean
+                if paired(n):
+                    for e in range(2):
+                        for g in range(8):
+                            for r in range(2):
+                                nc.tensor.matmul(
+                                    mean[:, e, g * 32:(g + 1) * 32], lhsT=H[n]["q2"][:, g, r, e::2], rhs=poolm2[:],
+                                    start=(r == 0), stop=(r == 1),
+                                )
+                    return
                 for u in range(2):
                     for bh in range(16):
                         nc.tensor.matmul(
@@ -151,7 +182,47 @@ def tile_attngate_kernel(tc, q, k, attention_mask, cos, sin, wq, wk, out):
         def copy(n, b):
             return None
 
+        def turn(n, g4):
+            tw = T(psum1, [P, 4, P], F32, "tw%d" % g4)
+            for i in range(4):
+                nc.tensor.matmul(tw[:, i, :], lhsT=H[n]["m1"][:, 4 * g4 + i, :].bitcast(F32), rhs=permp[:],
+                                 is_transpose=True, start=True, stop=True)
+            hc = T(two, [P, 4, P // 2], F32, "hc")
+            nc.scalar.copy(out=hc[:], in_=tw[:, :, P // 2:P])
+            H[n]["tw%d" % g4], H[n]["hc%d" % g4] = tw, hc
+
+        def pair_max(n, g4):
+            if g4 == 0:
+                H[n]["m2"] = T(two, [P, 8, P], BF16, "mp2")
+            tw = H[n]["tw%d" % g4][:].rearrange("p g q -> p (g q)").bitcast(BF16).rearrange("p (g q) -> p g q", g=4)
+            hc = H[n]["hc%d" % g4][:].rearrange("p g q -> p (g q)").bitcast(BF16).rearrange("p (g q) -> p g q", g=4)
+            nc.vector.tensor_tensor(out=H[n]["m2"][:, 4 * g4:4 * g4 + 4, :], in0=tw[:, :, 0:P], in1=hc, op=ALU.max)
+
+        def lev1_paired(n, b):
+            if b == 0:
+                q2 = H[n]["q2"]
+                m1 = T(two, [P, 8, D], BF16, "m1")
+                nc.vector.tensor_tensor(out=m1[:], in0=q2[:, :, 0, :], in1=q2[:, :, 1, :], op=ALU.max)
+                H[n]["m1"] = m1
+                turn(n, 0)
+                turn(n, 1)
+            elif b == 1:
+                pair_max(n, 0)
+            elif b == 2:
+                pair_max(n, 1)
+            else:
+                m2 = H[n]["m2"]
+                z = T(three, [P, 2, HB], F32, "z")
+                nc.vector.tensor_tensor(
+                    out=z[:, 1, :].bitcast(BF16).rearrange("p (g q) -> p g q", g=8),
+                    in0=m2[:, :, 0:P // 2], in1=m2[:, :, P // 2:P], op=ALU.max,
+                )
+                H[n]["z"] = z
+
         def lev1(n, b):
+            if paired(n):
+                lev1_paired(n, b)
+                return
             qa = H[n]["qa"]
             if b == 0:
                 m1 = T(two, [P, 2, 4, D], BF16, "m1")
@@ -166,13 +237,15 @@ def tile_attngate_kernel(tc, q, k, attention_mask, cos, sin, wq, wk, out):
                 m2 = H[n]["m2"]
                 m3 = T(two, [P, 2, D], BF16, "m3")
                 nc.vector.tensor_tensor(out=m3[:], in0=m2[:, :, 0, :], in1=m2[:, :, 1, :], op=ALU.max)
-                mt = T(psum1, [P, 2, P], F32, "mt")
+                mt = T(psum1, [P, 2, P], F32, "tw0")
                 for c in range(2):
                     nc.tensor.matmul(mt[:, c, :], lhsT=m3[:, c, :].bitcast(F32), rhs=identf[:], is_transpose=True,
                                      start=True, stop=True)
                 H[n]["mt"] = mt
 
         def lev23(n):
+            if paired(n):
+                return
             z = T(three, [P, 2, HB], F32, "z")
             nc.scalar.copy(out=z[:, 1, :], in_=H[n]["mt"][:].rearrange("p c b -> p (c b)"))
             H[n]["z"] = z

@@ -21,9 +21,7 @@ G = HQ // HK
 HB = NB // 2
 FLOPS = 2 * NB * (2 * D) * HID * (HQ + HK) + 2 * NB * NB * HID * HQ
 SCALE = 1.0 / math.sqrt(HID)
-MANUAL = False
-PAIRED = (1, 3)
-ADD_ON_G = False
+PAIRED = (0, 1)
 
 
 def tile_attngate_kernel(tc, q, k, attention_mask, cos, sin, wq, wk, out):
@@ -36,8 +34,7 @@ def tile_attngate_kernel(tc, q, k, attention_mask, cos, sin, wq, wk, out):
     NU = 2 * len(streams)
 
     with ExitStack() as ctx:
-        if MANUAL:
-            ctx.enter_context(tc.manual_schedule())
+        ctx.enter_context(tc.manual_schedule())
         const = ctx.enter_context(tc.tile_pool(name="const", bufs=1))
         qpool = ctx.enter_context(tc.tile_pool(name="qpool", bufs=5))
         two = ctx.enter_context(tc.tile_pool(name="two", bufs=2))
@@ -55,58 +52,65 @@ def tile_attngate_kernel(tc, q, k, attention_mask, cos, sin, wq, wk, out):
             YK.append((ykc, yks))
 
         ident = const.tile([P, P], BF16)
+        identf = const.tile([P, P], F32)
         pool32 = const.tile([P, P // BS], F32)
         poolm = const.tile([P, P // BS], BF16)
         pool32b = const.tile([P, P // 4], F32)
         poolm2 = const.tile([P, P // 4], BF16)
         permp = const.tile([P, P], F32)
         cs = const.tile([P, 4, 2, HID], BF16)
-        sraw = const.tile([P, 4, HID], BF16)
-        identf = const.tile([P, P], F32)
+        sraw = const.tile([P, 4, D], BF16)
         mbias = const.tile([P, 4, NB], F32)
         mw = const.tile([P, 4, NB, 2], I32)
+
+        def T(pool, shape, dtype, tag, **kw):
+            return pool.tile(shape, dtype, tag=tag, name=tag, **kw)
+
+        def ok(n):
+            return 0 <= n < NU
+
+        def isq(n):
+            return ok(n) and streams[n // 2][3] is not None
+
+        def paired(n):
+            return (n // 2) % 5 in PAIRED
+
+        def hs_of(n):
+            return slice((n % 2) * HB, (n % 2 + 1) * HB)
 
         def consts():
             make_identity(nc, ident[:])
             make_identity(nc, identf[:])
-            nc.vector.tensor_reduce(
-                out=pool32[:], in_=ident[:].rearrange("p (b j) -> p b j", j=BS), axis=AX.X, op=ALU.add
-            )
-            nc.vector.tensor_scalar(out=poolm[:], in0=pool32[:], scalar1=1.0 / BS, scalar2=None, op0=ALU.mult)
-            nc.vector.tensor_reduce(
-                out=pool32b[:], in_=ident[:].rearrange("p (b j) -> p b j", j=4), axis=AX.X, op=ALU.add
-            )
-            nc.vector.tensor_scalar(out=poolm2[:], in0=pool32b[:], scalar1=1.0 / BS, scalar2=None, op0=ALU.mult)
             nc.vector.tensor_copy(
                 out=permp[:].rearrange("p (j b) -> p j b", j=4), in_=identf[:].rearrange("p (b j) -> p j b", j=4)
             )
+            nc.vector.tensor_reduce(
+                out=pool32b[:], in_=ident[:].rearrange("p (b j) -> p b j", j=4), axis=AX.X, op=ALU.add
+            )
+            nc.vector.tensor_reduce(
+                out=pool32[:], in_=ident[:].rearrange("p (b j) -> p b j", j=BS), axis=AX.X, op=ALU.add
+            )
+            nc.vector.tensor_scalar(out=poolm2[:], in0=pool32b[:], scalar1=1.0 / BS, scalar2=None, op0=ALU.mult)
+            nc.vector.tensor_scalar(out=poolm[:], in0=pool32[:], scalar1=1.0 / BS, scalar2=None, op0=ALU.mult)
 
-        def load_tables():
-            nc.sync.dma_start(out=cs[:, :, 0, :], in_=cos[0].rearrange("(c p) h -> p c h", p=P))
-            nc.sync.dma_start(out=sraw[:], in_=sin[0].rearrange("(c p) h -> p c h", p=P))
+        def load_tables(hh):
+            c = slice(2 * hh, 2 * hh + 2)
+            rows = sin[0].rearrange("(c p) h -> p c h", p=P)
+            nc.sync.dma_start(out=cs[:, c, 0, :], in_=cos[0].rearrange("(c p) h -> p c h", p=P)[:, c, :])
+            nc.sync.dma_start(out=cs[:, c, 1, 0:D], in_=rows[:, c, D:HID])
+            nc.sync.dma_start(out=sraw[:, c, :], in_=rows[:, c, 0:D])
+            nc.gpsimd.tensor_scalar(
+                out=cs[:, c, 1, D:HID], in0=sraw[:, c, :], scalar1=-1.0, scalar2=0.0, op0=ALU.mult, op1=ALU.add
+            )
 
         def load_mask():
             mi = attention_mask.rearrange("a b i j -> (a b i) j").bitcast(I32)
-            assert mi.shape[1] == 2 * NB, "mask dtype %s" % str(attention_mask.dtype)
             nc.sync.dma_start(out=mw[:].rearrange("p c j e -> p c (j e)"), in_=mi.rearrange("(c p) w -> p c w", p=P))
-
-        def tables():
-            nc.scalar.copy(out=cs[:, :, 1, 0:D], in_=sraw[:, :, D:HID])
-            nc.scalar.mul(out=cs[:, :, 1, D:HID], in_=sraw[:, :, 0:D], mul=-1.0)
 
         def maskprep():
             nc.vector.tensor_scalar(
                 out=mbias[:], in0=mw[:, :, :, 0], scalar1=-1.0, scalar2=1.0e9, op0=ALU.add, op1=ALU.mult
             )
-
-        def T(pool, shape, dtype, tag, **kw):
-            return pool.tile(shape, dtype, tag=tag, name=tag, **kw)
-
-        def hs_of(n):
-            return slice((n % 2) * HB, (n % 2 + 1) * HB)
-
-        def paired(n):
-            return (n // 2) % 5 in PAIRED
 
         def load(n):
             x = streams[n // 2][0]
@@ -136,9 +140,13 @@ def tile_attngate_kernel(tc, q, k, attention_mask, cos, sin, wq, wk, out):
             )
             W[s]["wr"] = wr
 
-        def regroup(dst, src):
+        def rg_w(j):
+            s = j // 2
+            if j % 2 == 0:
+                W[s]["wg"] = T(two, [P, HID, 4], BF16, "wg", align_bytes=64)
             nc.scalar.copy(
-                out=dst.rearrange("p (c i) t -> p c t i", i=4), in_=src.rearrange("p t (c i) -> p c t i", i=4)
+                out=W[s]["wg"][:, hs_of(j), :].rearrange("p (c i) t -> p c t i", i=4),
+                in_=W[s]["wr"][:, :, hs_of(j)].rearrange("p t (c i) -> p c t i", i=4),
             )
 
         def quantise(grouped, codes, scales):
@@ -146,115 +154,98 @@ def tile_attngate_kernel(tc, q, k, attention_mask, cos, sin, wq, wk, out):
                 out=codes.bitcast(FP8X4), scales=scales, in_=grouped[:].rearrange("p n t -> p (n t)")
             )
 
-        def rg_w(j):
-            s = j // 2
-            if j % 2 == 0:
-                W[s]["wg"] = T(two, [P, HID, 4], BF16, "wg", align_bytes=64)
-            regroup(W[s]["wg"][:, hs_of(j), :], W[s]["wr"][:, :, hs_of(j)])
+        def q_w(s):
+            W[s]["wc"] = T(two, [P, HID], U32, "wc", align_bytes=64)
+            W[s]["ws"] = T(two, [P, HID], U8, "ws", align_bytes=64)
+            quantise(W[s]["wg"], W[s]["wc"][:], W[s]["ws"][:])
 
-        def q_w(j):
-            s = j // 2
-            if j % 2 == 1:
-                W[s]["wc"] = T(two, [P, HID], U32, "wc", align_bytes=64)
-                W[s]["ws"] = T(two, [P, HID], U8, "ws", align_bytes=64)
-                quantise(W[s]["wg"], W[s]["wc"][:], W[s]["ws"][:])
-
-        def bank(n, b):
-            if b == 0:
-                mean = T(psum1, [P, 2, HB], F32, "mean")
-                H[n]["mean"] = mean
+        def means(n):
+            mean = T(psum1, [P, 2, HB], F32, "mean")
+            H[n]["mean"] = mean
+            for e in range(2):
                 if paired(n):
-                    for e in range(2):
-                        for g in range(8):
-                            for r in range(2):
-                                nc.tensor.matmul(
-                                    mean[:, e, g * 32:(g + 1) * 32], lhsT=H[n]["q2"][:, g, r, e::2], rhs=poolm2[:],
-                                    start=(r == 0), stop=(r == 1),
-                                )
-                    return
-                for u in range(2):
+                    for g in range(8):
+                        for r in range(2):
+                            nc.tensor.matmul(
+                                mean[:, e, g * 32:(g + 1) * 32], lhsT=H[n]["q2"][:, g, r, e::2], rhs=poolm2[:],
+                                start=(r == 0), stop=(r == 1),
+                            )
+                else:
                     for bh in range(16):
                         nc.tensor.matmul(
-                            mean[:, u, bh * 16:(bh + 1) * 16], lhsT=H[n]["qp"][:, bh, u::2],
-                            rhs=poolm[:], start=True, stop=True,
+                            mean[:, e, bh * 16:(bh + 1) * 16], lhsT=H[n]["qp"][:, bh, e::2], rhs=poolm[:],
+                            start=True, stop=True,
                         )
 
-        def copy(n, b):
-            return None
-
-        def turn(n, g4):
-            tw = T(psum1, [P, 4, P], F32, "tw%d" % g4)
-            for i in range(4):
-                nc.tensor.matmul(tw[:, i, :], lhsT=H[n]["m1"][:, 4 * g4 + i, :].bitcast(F32), rhs=permp[:],
-                                 is_transpose=True, start=True, stop=True)
-            hc = T(two, [P, 4, P // 2], F32, "hc")
-            nc.scalar.copy(out=hc[:], in_=tw[:, :, P // 2:P])
-            H[n]["tw%d" % g4], H[n]["hc%d" % g4] = tw, hc
-
-        def pair_max(n, g4):
-            if g4 == 0:
-                H[n]["m2"] = T(two, [P, 8, P], BF16, "mp2")
-            tw = H[n]["tw%d" % g4][:].rearrange("p g q -> p (g q)").bitcast(BF16).rearrange("p (g q) -> p g q", g=4)
-            hc = H[n]["hc%d" % g4][:].rearrange("p g q -> p (g q)").bitcast(BF16).rearrange("p (g q) -> p g q", g=4)
-            nc.vector.tensor_tensor(out=H[n]["m2"][:, 4 * g4:4 * g4 + 4, :], in0=tw[:, :, 0:P], in1=hc, op=ALU.max)
-
-        def lev1_paired(n, b):
-            if b == 0:
-                q2 = H[n]["q2"]
-                m1 = T(two, [P, 8, D], BF16, "m1")
-                nc.vector.tensor_tensor(out=m1[:], in0=q2[:, :, 0, :], in1=q2[:, :, 1, :], op=ALU.max)
-                H[n]["m1"] = m1
-                turn(n, 0)
-                turn(n, 1)
-            elif b == 1:
-                pair_max(n, 0)
-            elif b == 2:
-                pair_max(n, 1)
-            else:
-                m2 = H[n]["m2"]
-                z = T(three, [P, 2, HB], F32, "z")
-                nc.vector.tensor_tensor(
-                    out=z[:, 1, :].bitcast(BF16).rearrange("p (g q) -> p g q", g=8),
-                    in0=m2[:, :, 0:P // 2], in1=m2[:, :, P // 2:P], op=ALU.max,
-                )
-                H[n]["z"] = z
-
-        def lev1(n, b):
-            if paired(n):
-                lev1_paired(n, b)
-                return
-            qa = H[n]["qa"]
-            if b == 0:
-                m1 = T(two, [P, 2, 4, D], BF16, "m1")
-                nc.vector.tensor_tensor(out=m1[:], in0=qa[:, :, 0:4, :], in1=qa[:, :, 4:8, :], op=ALU.max)
-                H[n]["m1"] = m1
-            elif b == 1:
-                m1 = H[n]["m1"]
-                m2 = T(two, [P, 2, 2, D], BF16, "mx2")
-                nc.vector.tensor_tensor(out=m2[:], in0=m1[:, :, 0:2, :], in1=m1[:, :, 2:4, :], op=ALU.max)
-                H[n]["m2"] = m2
-            elif b == 2:
-                m2 = H[n]["m2"]
-                m3 = T(two, [P, 2, D], BF16, "m3")
-                nc.vector.tensor_tensor(out=m3[:], in0=m2[:, :, 0, :], in1=m2[:, :, 1, :], op=ALU.max)
-                mt = T(psum1, [P, 2, P], F32, "tw0")
-                for c in range(2):
-                    nc.tensor.matmul(mt[:, c, :], lhsT=m3[:, c, :].bitcast(F32), rhs=identf[:], is_transpose=True,
-                                     start=True, stop=True)
-                H[n]["mt"] = mt
-
-        def lev23(n):
-            if paired(n):
-                return
-            z = T(three, [P, 2, HB], F32, "z")
-            nc.scalar.copy(out=z[:, 1, :], in_=H[n]["mt"][:].rearrange("p c b -> p (c b)"))
-            H[n]["z"] = z
-
         def mevac(n):
+            H[n]["z"] = T(three, [P, 2, HB], F32, "z")
             nc.scalar.copy(
                 out=H[n]["z"][:, 0, :].bitcast(BF16).rearrange("p (b e) -> p b e", e=2),
                 in_=H[n]["mean"][:].rearrange("p e b -> p b e"),
             )
+
+        def max_a(n):
+            m1 = T(two, [P, 2, 4, D], BF16, "m1")
+            if paired(n):
+                q2 = H[n]["q2"]
+                nc.vector.tensor_tensor(
+                    out=m1[:].rearrange("p c j f -> p (c j) f"), in0=q2[:, :, 0, :], in1=q2[:, :, 1, :], op=ALU.max
+                )
+            else:
+                qa = H[n]["qa"]
+                nc.vector.tensor_tensor(out=m1[:], in0=qa[:, :, 0:4, :], in1=qa[:, :, 4:8, :], op=ALU.max)
+            H[n]["m1"] = m1
+
+        def turn(n, g4):
+            rows = H[n]["m1"][:].rearrange("p c j f -> p (c j) f")
+            tw = T(psum1, [P, 4, P], F32, "tw%d" % g4)
+            for i in range(4):
+                nc.tensor.matmul(tw[:, i, :], lhsT=rows[:, 4 * g4 + i, :].bitcast(F32), rhs=permp[:],
+                                 is_transpose=True, start=True, stop=True)
+            H[n]["tw%d" % g4] = tw
+
+        def half(n, g4):
+            hc = T(two, [P, 4, P // 2], F32, "hc")
+            nc.scalar.copy(out=hc[:], in_=H[n]["tw%d" % g4][:, :, P // 2:P])
+            H[n]["hc%d" % g4] = hc
+
+        def max_b(n):
+            if paired(n):
+                H[n]["m2"] = T(two, [P, 8, P], BF16, "mp2")
+                for g4 in range(2):
+                    tw = H[n]["tw%d" % g4][:].rearrange("p g q -> p (g q)").bitcast(BF16)
+                    hc = H[n]["hc%d" % g4][:].rearrange("p g q -> p (g q)").bitcast(BF16)
+                    nc.vector.tensor_tensor(
+                        out=H[n]["m2"][:, 4 * g4:4 * g4 + 4, :], in0=tw.rearrange("p (g q) -> p g q", g=4)[:, :, 0:P],
+                        in1=hc.rearrange("p (g q) -> p g q", g=4), op=ALU.max,
+                    )
+                return
+            m1 = H[n]["m1"]
+            m2 = T(two, [P, 2, 2, D], BF16, "mx2")
+            nc.vector.tensor_tensor(out=m2[:], in0=m1[:, :, 0:2, :], in1=m1[:, :, 2:4, :], op=ALU.max)
+            H[n]["m2"] = m2
+
+        def max_c(n):
+            m2 = H[n]["m2"]
+            if paired(n):
+                nc.vector.tensor_tensor(
+                    out=H[n]["z"][:, 1, :].bitcast(BF16).rearrange("p (g q) -> p g q", g=8),
+                    in0=m2[:, :, 0:P // 2], in1=m2[:, :, P // 2:P], op=ALU.max,
+                )
+                return
+            m3 = T(two, [P, 2, D], BF16, "m3")
+            nc.vector.tensor_tensor(out=m3[:], in0=m2[:, :, 0, :], in1=m2[:, :, 1, :], op=ALU.max)
+            H[n]["m3"] = m3
+
+        def turn_max(n):
+            mt = T(psum1, [P, 2, P], F32, "tw0")
+            for c in range(2):
+                nc.tensor.matmul(mt[:, c, :], lhsT=H[n]["m3"][:, c, :].bitcast(F32), rhs=identf[:], is_transpose=True,
+                                 start=True, stop=True)
+            H[n]["mt"] = mt
+
+        def max_evac(n):
+            nc.scalar.copy(out=H[n]["z"][:, 1, :], in_=H[n]["mt"][:].rearrange("p c b -> p (c b)"))
 
         def rg_z(n):
             pg = T(two, [P, HB, 4], BF16, "pg", align_bytes=64)
@@ -269,39 +260,40 @@ def tile_attngate_kernel(tc, q, k, attention_mask, cos, sin, wq, wk, out):
             H[n]["ps"] = T(two, [P, HB], U8, "ps", align_bytes=64)
             quantise(H[n]["pg"], H[n]["pc"][:], H[n]["ps"][:])
 
-        def mx(n):
-            wc, ws = W[n // 2]["wc"], W[n // 2]["ws"]
-            for cc in range(2):
-                x = T(psum, [P, HID], F32, "x")
-                nc.tensor.matmul_mx(
-                    out=x[:],
-                    lhsT=H[n]["pc"][:, cc * P:(cc + 1) * P].bitcast(FP8X4), lhsT_scale=H[n]["ps"][:, cc * P:(cc + 1) * P],
-                    rhs=wc[:].bitcast(FP8X4), rhs_scale=ws[:], start=True, stop=True,
-                )
-                H[n]["x%d" % cc] = x
+        def mx(n, cc):
+            x = T(psum, [P, HID], F32, "x")
+            nc.tensor.matmul_mx(
+                out=x[:],
+                lhsT=H[n]["pc"][:, cc * P:(cc + 1) * P].bitcast(FP8X4), lhsT_scale=H[n]["ps"][:, cc * P:(cc + 1) * P],
+                rhs=W[n // 2]["wc"][:].bitcast(FP8X4), rhs_scale=W[n // 2]["ws"][:], start=True, stop=True,
+            )
+            H[n]["x%d" % cc] = x
 
-        def mult(n, i):
-            if i % 2 == 1:
-                return None
-            cc = i // 2
-            x = H[n]["x%d" % cc]
-            if i == 0:
-                H[n]["yg"] = T(three, [P, HB, 4], BF16, "yg", align_bytes=64)
+        def mult(n, cc):
             ab = T(three, [P, 2, HID], F32, "ab")
             nc.vector.tensor_tensor(
-                out=ab[:], in0=x[:].unsqueeze(1).to_broadcast([P, 2, HID]), in1=cs[:, 2 * (n % 2) + cc], op=ALU.mult
+                out=ab[:], in0=H[n]["x%d" % cc][:].unsqueeze(1).to_broadcast([P, 2, HID]),
+                in1=cs[:, 2 * (n % 2) + cc], op=ALU.mult,
             )
-            yt = T(psum, [P, 4, P], F32, "yt")
+            H[n]["ab%d" % cc] = ab
+
+        def rope(n, cc):
+            ab = H[n]["ab%d" % cc]
+            yt = T(psum1, [P, 4, P], F32, "yt")
             for m in range(4):
                 mo = (m + 2) % 4
                 nc.tensor.matmul(yt[:, m, :], lhsT=ab[:, 0, m * P:(m + 1) * P], rhs=identf[:], is_transpose=True,
                                  start=True, stop=False)
                 nc.tensor.matmul(yt[:, m, :], lhsT=ab[:, 1, mo * P:(mo + 1) * P], rhs=identf[:], is_transpose=True,
                                  start=False, stop=True)
-            nc.scalar.copy(out=H[n]["yg"][:, cc * P:(cc + 1) * P, :], in_=yt[:].rearrange("p m b -> p b m"))
+            H[n]["yt%d" % cc] = yt
 
-        def add(n):
-            return None
+        def yevac(n, cc):
+            if cc == 0:
+                H[n]["yg"] = T(three, [P, HB, 4], BF16, "yg", align_bytes=64)
+            nc.scalar.copy(
+                out=H[n]["yg"][:, cc * P:(cc + 1) * P, :], in_=H[n]["yt%d" % cc][:].rearrange("p m b -> p b m")
+            )
 
         def q_y(n):
             kv, h = streams[n // 2][2], streams[n // 2][3]
@@ -314,7 +306,7 @@ def tile_attngate_kernel(tc, q, k, attention_mask, cos, sin, wq, wk, out):
 
         def score(n, cc):
             kv = streams[n // 2][2]
-            sc = T(psum1, [P, NB], F32, "sc")
+            sc = T(psum, [P, NB], F32, "sc")
             nc.tensor.matmul_mx(
                 out=sc[:],
                 lhsT=H[n]["yc"][:, cc * P:(cc + 1) * P].bitcast(FP8X4), lhsT_scale=H[n]["ys"][:, cc * P:(cc + 1) * P],
@@ -357,70 +349,87 @@ def tile_attngate_kernel(tc, q, k, attention_mask, cos, sin, wq, wk, out):
                 out=out[0, h, hs_of(n), :].rearrange("(c p) j -> p c j", p=P), in_=H[n]["t2"][:]
             )
 
-        def ok(n):
-            return 0 <= n < NU
-
-        def isq(n):
-            return ok(n) and streams[n // 2][3] is not None
-
-        consts()
         load(0)
         load_w(0)
+        consts()
+        load_tables(0)
         load(1)
-        load_tables()
+        load_tables(1)
         load_w(1)
         load(2)
-        load_mask()
+        load_w(2)
         load(3)
+        load_mask()
         for t in range(NU + 5):
+            if t % 2 == 1 and (t + 5) // 2 < len(streams):
+                load_w((t + 5) // 2)
             if ok(t + 4):
                 load(t + 4)
-            if t % 2 == 0 and t // 2 + 2 < len(streams):
-                load_w(t // 2 + 2)
             if ok(t - 1):
                 rg_z(t - 1)
-            if t == 1:
-                q_w(0)
-            if ok(t) and t >= 1:
-                q_w(t)
+            if isq(t - 4):
+                expo(t - 4, 0)
+                expo(t - 4, 1)
+            if ok(t):
+                max_a(t)
+                means(t)
             if ok(t - 3):
                 q_y(t - 3)
-            for b in range(4):
-                if ok(t):
-                    bank(t, b)
-                    copy(t, b)
-                if ok(t - 2):
-                    mult(t - 2, b)
-                if ok(t):
-                    lev1(t, b)
-                if b < 2 and isq(t - 4):
-                    expo(t - 4, b)
-                if b == 1 and isq(t - 3):
-                    score(t - 3, 0)
-                    score(t - 3, 1)
-            if ok(t - 2):
-                add(t - 2)
             if isq(t - 3):
-                stt(t - 3, 0)
-                stt(t - 3, 1)
-                red(t - 3)
-            if ok(t - 1):
-                q_p(t - 1)
-                mx(t - 1)
+                score(t - 3, 0)
+                score(t - 3, 1)
             if ok(t):
-                lev23(t)
+                if paired(t):
+                    turn(t, 0)
+                    turn(t, 1)
+                    half(t, 0)
+                    half(t, 1)
                 mevac(t)
-            if isq(t - 4):
-                rec(t - 4)
             if t == 0:
                 rg_w(0)
-            if ok(t + 1):
-                rg_w(t + 1)
+                rg_w(1)
+            if t > 1 and ok(t + 2):
+                rg_w(t + 2)
+            if ok(t - 2):
+                mult(t - 2, 0)
+                rope(t - 2, 0)
+                yevac(t - 2, 0)
+            if ok(t - 1):
+                q_p(t - 1)
+                mx(t - 1, 0)
+            if isq(t - 3):
+                stt(t - 3, 0)
             if isq(t - 4):
+                rec(t - 4)
                 norm(t - 4, 0)
                 norm(t - 4, 1)
                 store(t - 4)
+            if ok(t - 2):
+                mult(t - 2, 1)
+                rope(t - 2, 1)
+            if ok(t - 1):
+                mx(t - 1, 1)
+            if ok(t - 2):
+                yevac(t - 2, 1)
+            if ok(t):
+                max_b(t)
+            if isq(t - 3):
+                stt(t - 3, 1)
+            if t == 2:
+                q_w(1)
+            if t % 2 == 1 and t > 1 and (t + 1) // 2 < len(streams):
+                q_w((t + 1) // 2)
+            if ok(t):
+                max_c(t)
+                if not paired(t):
+                    turn_max(t)
+                    max_evac(t)
             if t == 0:
-                tables()
-            if t == 3:
+                q_w(0)
+            if isq(t - 3):
+                red(t - 3)
+            if t == 1:
+                rg_w(2)
+                rg_w(3)
+            if t == 4:
                 maskprep()

@@ -21,7 +21,7 @@ G = HQ // HK
 HB = NB // 2
 FLOPS = 2 * NB * (2 * D) * HID * (HQ + HK) + 2 * NB * NB * HID * HQ
 SCALE = 1.0 / math.sqrt(HID)
-PAIRED = (0, 1)
+PAIRED = (0, 1, 4, 7)
 
 
 def tile_attngate_kernel(tc, q, k, attention_mask, cos, sin, wq, wk, out):
@@ -73,7 +73,7 @@ def tile_attngate_kernel(tc, q, k, attention_mask, cos, sin, wq, wk, out):
             return ok(n) and streams[n // 2][3] is not None
 
         def paired(n):
-            return (n // 2) % 5 in PAIRED
+            return n // 2 in PAIRED
 
         def hs_of(n):
             return slice((n % 2) * HB, (n % 2 + 1) * HB)

@@ -21,7 +21,7 @@ G = HQ // HK
 HB = NB // 2
 FLOPS = 2 * NB * (2 * D) * HID * (HQ + HK) + 2 * NB * NB * HID * HQ
 SCALE = 1.0 / math.sqrt(HID)
-PAIRED = (0, 1, 4, 7)
+PAIRED = (0, 1, 2, 6)
 
 
 def tile_attngate_kernel(tc, q, k, attention_mask, cos, sin, wq, wk, out):
@@ -61,6 +61,8 @@ def tile_attngate_kernel(tc, q, k, attention_mask, cos, sin, wq, wk, out):
         cs = const.tile([P, 4, 2, HID], BF16)
         sraw = const.tile([P, 4, D], BF16)
         mbias = const.tile([P, 4, NB], F32)
+        mbt = const.tile([P, 4, NB], F32)
+        minus1 = const.tile([P, 2], F32)
         mw = const.tile([P, 4, NB, 2], I32)
 
         def T(pool, shape, dtype, tag, **kw):
@@ -81,6 +83,7 @@ def tile_attngate_kernel(tc, q, k, attention_mask, cos, sin, wq, wk, out):
         def consts():
             make_identity(nc, ident[:])
             make_identity(nc, identf[:])
+            nc.gpsimd.memset(minus1[:], -1.0)
             nc.vector.tensor_copy(
                 out=permp[:].rearrange("p (j b) -> p j b", j=4), in_=identf[:].rearrange("p (b j) -> p j b", j=4)
             )
@@ -112,6 +115,14 @@ def tile_attngate_kernel(tc, q, k, attention_mask, cos, sin, wq, wk, out):
                 out=mbias[:], in0=mw[:, :, :, 0], scalar1=-1.0, scalar2=1.0e9, op0=ALU.add, op1=ALU.mult
             )
 
+        def mask_turn():
+            for kc in range(4):
+                sc = T(psum, [P, NB], F32, "sc")
+                for c in range(4):
+                    nc.tensor.matmul(sc[:, c * P:(c + 1) * P], lhsT=mbias[:, c, kc * P:(kc + 1) * P], rhs=identf[:],
+                                     is_transpose=True, start=True, stop=True)
+                nc.scalar.copy(out=mbt[:, kc, :], in_=sc[:])
+
         def load(n):
             x = streams[n // 2][0]
             if paired(n):
@@ -140,11 +151,11 @@ def tile_attngate_kernel(tc, q, k, attention_mask, cos, sin, wq, wk, out):
             )
             W[s]["wr"] = wr
 
-        def rg_w(j):
+        def rg_w(j, copy=nc.scalar.copy):
             s = j // 2
             if j % 2 == 0:
                 W[s]["wg"] = T(two, [P, HID, 4], BF16, "wg", align_bytes=64)
-            nc.scalar.copy(
+            copy(
                 out=W[s]["wg"][:, hs_of(j), :].rearrange("p (c i) t -> p c t i", i=4),
                 in_=W[s]["wr"][:, :, hs_of(j)].rearrange("p t (c i) -> p c t i", i=4),
             )
@@ -160,7 +171,10 @@ def tile_attngate_kernel(tc, q, k, attention_mask, cos, sin, wq, wk, out):
             quantise(W[s]["wg"], W[s]["wc"][:], W[s]["ws"][:])
 
         def means(n):
-            mean = T(psum1, [P, 2, HB], F32, "mean")
+            if paired(n):
+                mean = T(psum1, [P, 2, HB], F32, "mean")
+            else:
+                mean = T(psum1, [P, 4, HB], BF16, "mean")
             H[n]["mean"] = mean
             for e in range(2):
                 if paired(n):
@@ -238,21 +252,21 @@ def tile_attngate_kernel(tc, q, k, attention_mask, cos, sin, wq, wk, out):
             H[n]["m3"] = m3
 
         def turn_max(n):
-            mt = T(psum1, [P, 2, P], F32, "tw0")
             for c in range(2):
-                nc.tensor.matmul(mt[:, c, :], lhsT=H[n]["m3"][:, c, :].bitcast(F32), rhs=identf[:], is_transpose=True,
-                                 start=True, stop=True)
-            H[n]["mt"] = mt
-
-        def max_evac(n):
-            nc.scalar.copy(out=H[n]["z"][:, 1, :], in_=H[n]["mt"][:].rearrange("p c b -> p (c b)"))
+                for e in range(2):
+                    nc.tensor.transpose(
+                        H[n]["mean"][:, 2 + e, c * P:(c + 1) * P], H[n]["m3"][:, c, e::2], ident[:]
+                    )
 
         def rg_z(n):
             pg = T(two, [P, HB, 4], BF16, "pg", align_bytes=64)
-            nc.scalar.copy(
-                out=pg[:].rearrange("p b t -> p (b t)").bitcast(F32).rearrange("p (b s) -> p b s", s=2),
-                in_=H[n]["z"][:].rearrange("p s b -> p b s"),
-            )
+            if paired(n):
+                nc.scalar.copy(
+                    out=pg[:].rearrange("p b t -> p (b t)").bitcast(F32).rearrange("p (b s) -> p b s", s=2),
+                    in_=H[n]["z"][:].rearrange("p s b -> p b s"),
+                )
+            else:
+                nc.scalar.copy(out=pg[:], in_=H[n]["mean"][:].rearrange("p t b -> p b t"))
             H[n]["pg"] = pg
 
         def q_p(n):
@@ -261,7 +275,7 @@ def tile_attngate_kernel(tc, q, k, attention_mask, cos, sin, wq, wk, out):
             quantise(H[n]["pg"], H[n]["pc"][:], H[n]["ps"][:])
 
         def mx(n, cc):
-            x = T(psum, [P, HID], F32, "x")
+            x = T(psum1, [P, HID], F32, "tw%d" % cc if n == NU - 1 else "x")
             nc.tensor.matmul_mx(
                 out=x[:],
                 lhsT=H[n]["pc"][:, cc * P:(cc + 1) * P].bitcast(FP8X4), lhsT_scale=H[n]["ps"][:, cc * P:(cc + 1) * P],
@@ -304,50 +318,98 @@ def tile_attngate_kernel(tc, q, k, attention_mask, cos, sin, wq, wk, out):
                 H[n]["ys"] = T(three, [P, HB], U8, "ys", align_bytes=64)
                 quantise(H[n]["yg"], H[n]["yc"][:], H[n]["ys"][:])
 
-        def score(n, cc):
-            kv = streams[n // 2][2]
+        def score(n, i):
+            ykc, yks = YK[streams[n // 2][2]]
+            scT = T(psum1, [P, 2, HB], F32, "scT")
+            for r in range(2):
+                keys = slice((2 * i + r) * P, (2 * i + r + 1) * P)
+                nc.tensor.matmul_mx(
+                    out=scT[:, r, :], lhsT=ykc[:, keys].bitcast(FP8X4), lhsT_scale=yks[:, keys],
+                    rhs=H[n]["yc"][:].bitcast(FP8X4), rhs_scale=H[n]["ys"][:], start=True, stop=True,
+                )
+            H[n]["scT%d" % i] = scT
+
+        def sevac(n, i):
+            if i == 0:
+                H[n]["st"] = T(two, [P, 4, HB], F32, "st")
+            nc.scalar.activation(
+                out=H[n]["st"][:, 2 * i:2 * i + 2, :], in_=H[n]["scT%d" % i][:], func=ACT.Copy, scale=SCALE
+            )
+
+        def masked(n, cc):
+            c = 2 * (n % 2) + cc
+            sc = T(psum, [P, NB], F32, "sc")
+            for kc in range(4):
+                keys = slice(kc * P, (kc + 1) * P)
+                nc.tensor.matmul(sc[:, keys], lhsT=H[n]["st"][:, kc, cc * P:(cc + 1) * P], rhs=identf[:],
+                                 is_transpose=True, start=True, stop=False)
+                nc.tensor.matmul(sc[:, keys], lhsT=mbt[:, kc, c * P:(c + 1) * P], rhs=identf[:],
+                                 is_transpose=True, start=False, stop=True)
+            H[n]["sc%d" % cc] = sc[:]
+
+        def score_straight(n, cc):
+            ykc, yks = YK[streams[n // 2][2]]
+            rows = slice(cc * P, (cc + 1) * P)
             sc = T(psum, [P, NB], F32, "sc")
             nc.tensor.matmul_mx(
-                out=sc[:],
-                lhsT=H[n]["yc"][:, cc * P:(cc + 1) * P].bitcast(FP8X4), lhsT_scale=H[n]["ys"][:, cc * P:(cc + 1) * P],
-                rhs=YK[kv][0][:].bitcast(FP8X4), rhs_scale=YK[kv][1][:], start=True, stop=True,
+                out=sc[:], lhsT=H[n]["yc"][:, rows].bitcast(FP8X4), lhsT_scale=H[n]["ys"][:, rows],
+                rhs=ykc[:].bitcast(FP8X4), rhs_scale=yks[:], start=True, stop=True,
             )
-            H[n]["sc%d" % cc] = sc
+            H[n]["raw%d" % cc] = sc
 
         def stt(n, cc):
             if cc == 0:
-                H[n]["t2"] = T(four, [P, 2, NB], F32, "t2")
+                H[n]["t1"] = T(three, [P, 2, NB], F32, "ab")
             nc.vector.scalar_tensor_tensor(
-                out=H[n]["t2"][:, cc, :], in0=H[n]["sc%d" % cc][:], scalar=SCALE,
+                out=H[n]["t1"][:, cc, :], in0=H[n]["raw%d" % cc][:], scalar=SCALE,
                 in1=mbias[:, 2 * (n % 2) + cc, :], op0=ALU.mult, op1=ALU.add,
             )
+            H[n]["sc%d" % cc] = H[n]["t1"][:, cc, :]
 
-        def red(n):
-            H[n]["nmx"] = T(four, [P, 2], F32, "nmx")
-            nc.vector.tensor_reduce(out=H[n]["nmx"][:], in_=H[n]["t2"][:], axis=AX.X, op=ALU.max, negate=True)
+        def red(n, cc):
+            if cc == 0:
+                H[n]["nmx"] = T(four, [P, 2], F32, "nmx")
+            nc.vector.tensor_reduce(
+                out=H[n]["nmx"][:, cc:cc + 1], in_=H[n]["sc%d" % cc], axis=AX.X, op=ALU.max, negate=True
+            )
 
         def expo(n, cc):
             if cc == 0:
                 H[n]["ssum"] = T(four, [P, 2], F32, "ssum")
+                H[n]["t2"] = T(four, [P, 2, NB], F32, "t2")
             nc.scalar.activation(
-                out=H[n]["t2"][:, cc, :], in_=H[n]["t2"][:, cc, :], func=ACT.Exp,
+                out=H[n]["t2"][:, cc, :], in_=H[n]["sc%d" % cc], func=ACT.Exp,
                 bias=H[n]["nmx"][:, cc:cc + 1], scale=1.0, accum_out=H[n]["ssum"][:, cc:cc + 1],
             )
 
         def rec(n):
             H[n]["rs"] = T(four, [P, 2], F32, "rs")
-            nc.vector.reciprocal(out=H[n]["rs"][:], in_=H[n]["ssum"][:])
+            if n < NU - 2:
+                nc.gpsimd.tensor_tensor(out=H[n]["rs"][:], in0=H[n]["ssum"][:], in1=minus1[:], op=ALU.pow)
+            else:
+                nc.vector.reciprocal(out=H[n]["rs"][:], in_=H[n]["ssum"][:])
 
         def norm(n, cc):
-            nc.scalar.activation(
-                out=H[n]["t2"][:, cc, :], in_=H[n]["t2"][:, cc, :], func=ACT.Copy, scale=H[n]["rs"][:, cc:cc + 1]
+            nc.gpsimd.tensor_scalar(
+                out=H[n]["t2"][:, cc, :], in0=H[n]["t2"][:, cc, :], scalar1=H[n]["rs"][:, cc:cc + 1], scalar2=1.0,
+                op0=ALU.mult, op1=ALU.mult,
             )
 
         def store(n):
             h = streams[n // 2][3]
-            nc.scalar.dma_start(
+            nc.sync.dma_start(
                 out=out[0, h, hs_of(n), :].rearrange("(c p) j -> p c j", p=P), in_=H[n]["t2"][:]
             )
+
+        def softmax_head(n, cc):
+            red(n, cc)
+            expo(n, cc)
+
+        def finish(n):
+            rec(n)
+            norm(n, 0)
+            norm(n, 1)
+            store(n)
 
         load(0)
         load_w(0)
@@ -360,45 +422,58 @@ def tile_attngate_kernel(tc, q, k, attention_mask, cos, sin, wq, wk, out):
         load_w(2)
         load(3)
         load_mask()
-        for t in range(NU + 5):
+        for t in range(NU + 1):
             if t % 2 == 1 and (t + 5) // 2 < len(streams):
                 load_w((t + 5) // 2)
             if ok(t + 4):
                 load(t + 4)
+            if ok(t):
+                max_a(t)
+            if t == 0:
+                rg_w(0, nc.vector.tensor_copy)
+                rg_w(1, nc.vector.tensor_copy)
+            if ok(t) and paired(t):
+                turn(t, 0)
+                turn(t, 1)
             if ok(t - 1):
                 rg_z(t - 1)
             if isq(t - 4):
+                red(t - 4, 0)
                 expo(t - 4, 0)
-                expo(t - 4, 1)
-            if ok(t):
-                max_a(t)
-                means(t)
+            if ok(t) and paired(t):
+                half(t, 0)
+                half(t, 1)
             if ok(t - 3):
                 q_y(t - 3)
             if isq(t - 3):
                 score(t - 3, 0)
-                score(t - 3, 1)
+                sevac(t - 3, 0)
             if ok(t):
-                if paired(t):
-                    turn(t, 0)
-                    turn(t, 1)
-                    half(t, 0)
-                    half(t, 1)
+                means(t)
+            if isq(t - 4):
+                red(t - 4, 1)
+                expo(t - 4, 1)
+            if isq(t - 3):
+                score(t - 3, 1)
+                sevac(t - 3, 1)
+            if ok(t) and paired(t):
                 mevac(t)
-            if t == 0:
-                rg_w(0)
-                rg_w(1)
-            if t > 1 and ok(t + 2):
-                rg_w(t + 2)
             if ok(t - 2):
                 mult(t - 2, 0)
+                mx(t - 2, 1)
                 rope(t - 2, 0)
                 yevac(t - 2, 0)
             if ok(t - 1):
                 q_p(t - 1)
+            if t == NU:
                 mx(t - 1, 0)
+                mx(t - 1, 1)
             if isq(t - 3):
-                stt(t - 3, 0)
+                masked(t - 3, 0)
+            if t > 1 and ok(t + 2):
+                rg_w(t + 2)
+            if ok(t):
+                max_b(t)
             if isq(t - 4):
                 rec(t - 4)
                 norm(t - 4, 0)
@@ -407,29 +482,48 @@ def tile_attngate_kernel(tc, q, k, attention_mask, cos, sin, wq, wk, out):
             if ok(t - 2):
                 mult(t - 2, 1)
                 rope(t - 2, 1)
-            if ok(t - 1):
-                mx(t - 1, 1)
-            if ok(t - 2):
-                yevac(t - 2, 1)
-            if ok(t):
-                max_b(t)
-            if isq(t - 3):
-                stt(t - 3, 1)
-            if t == 2:
-                q_w(1)
-            if t % 2 == 1 and t > 1 and (t + 1) // 2 < len(streams):
-                q_w((t + 1) // 2)
+            if t % 2 == 0 and t // 2 < len(streams):
+                q_w(t // 2)
             if ok(t):
                 max_c(t)
                 if not paired(t):
                     turn_max(t)
-                    max_evac(t)
-            if t == 0:
-                q_w(0)
             if isq(t - 3):
-                red(t - 3)
+                masked(t - 3, 1)
+            if t < NU and ok(t - 1):
+                mx(t - 1, 0)
+            if ok(t - 2):
+                yevac(t - 2, 1)
             if t == 1:
-                rg_w(2)
-                rg_w(3)
-            if t == 4:
+                rg_w(2, nc.vector.tensor_copy)
+                rg_w(3, nc.vector.tensor_copy)
+            if t == 3:
                 maskprep()
+                mask_turn()
+
+        last = NU - 1
+        mult(last, 0)
+        rope(last, 0)
+        mult(last, 1)
+        rope(last, 1)
+        yevac(last, 0)
+        softmax_head(last - 2, 0)
+        q_y(last - 1)
+        score_straight(last - 1, 0)
+        score_straight(last - 1, 1)
+        softmax_head(last - 2, 1)
+        yevac(last, 1)
+        stt(last - 1, 0)
+        stt(last - 1, 1)
+        q_y(last)
+        score_straight(last, 0)
+        score_straight(last, 1)
+        finish(last - 2)
+        softmax_head(last - 1, 0)
+        softmax_head(last - 1, 1)
+        stt(last, 0)
+        stt(last, 1)
+        finish(last - 1)
+        softmax_head(last, 0)
+        softmax_head(last, 1)
+        finish(last)

@@ -329,6 +329,14 @@ def tile_attngate_kernel(tc, q, k, attention_mask, cos, sin, wq, wk, out):
                 )
             H[n]["scT%d" % i] = scT
 
+        def keep_warm(n):
+            idle = T(psum1, [P, NB], F32, "scT")
+            w = W[n // 2]
+            nc.tensor.matmul_mx(
+                out=idle[:], lhsT=w["wc"][:, 0:P].bitcast(FP8X4), lhsT_scale=w["ws"][:, 0:P],
+                rhs=w["wc"][:].bitcast(FP8X4), rhs_scale=w["ws"][:], start=True, stop=True,
+            )
+
         def sevac(n, i):
             if i == 0:
                 H[n]["st"] = T(two, [P, 4, HB], F32, "st")
@@ -470,6 +478,8 @@ def tile_attngate_kernel(tc, q, k, attention_mask, cos, sin, wq, wk, out):
                 mx(t - 1, 1)
             if isq(t - 3):
                 masked(t - 3, 0)
+                if t < NU:
+                    keep_warm(t - 2)
             if t > 1 and ok(t + 2):
                 rg_w(t + 2)
             if ok(t):
@@ -489,6 +499,8 @@ def tile_attngate_kernel(tc, q, k, attention_mask, cos, sin, wq, wk, out):
                 if not paired(t):
                     turn_max(t)
             if isq(t - 3):
+                if t < NU:
+                    keep_warm(t - 2)
                 masked(t - 3, 1)
             if t < NU and ok(t - 1):
                 mx(t - 1, 0)

@@ -62,7 +62,6 @@ def tile_attngate_kernel(tc, q, k, attention_mask, cos, sin, wq, wk, out):
         sraw = const.tile([P, 4, D], BF16)
         mbias = const.tile([P, 4, NB], F32)
         mbt = const.tile([P, 4, NB], F32)
-        minus1 = const.tile([P, 2], F32)
         mw = const.tile([P, 4, NB, 2], I32)
 
         def T(pool, shape, dtype, tag, **kw):
@@ -83,7 +82,6 @@ def tile_attngate_kernel(tc, q, k, attention_mask, cos, sin, wq, wk, out):
         def consts():
             make_identity(nc, ident[:])
             make_identity(nc, identf[:])
-            nc.gpsimd.memset(minus1[:], -1.0)
             nc.vector.tensor_copy(
                 out=permp[:].rearrange("p (j b) -> p j b", j=4), in_=identf[:].rearrange("p (b j) -> p j b", j=4)
             )
@@ -115,8 +113,8 @@ def tile_attngate_kernel(tc, q, k, attention_mask, cos, sin, wq, wk, out):
                 out=mbias[:], in0=mw[:, :, :, 0], scalar1=-1.0, scalar2=1.0e9, op0=ALU.add, op1=ALU.mult
             )
 
-        def mask_turn():
-            for kc in range(4):
+        def mask_turn(chunks):
+            for kc in chunks:
                 sc = T(psum, [P, NB], F32, "sc")
                 for c in range(4):
                     nc.tensor.matmul(sc[:, c * P:(c + 1) * P], lhsT=mbias[:, c, kc * P:(kc + 1) * P], rhs=identf[:],
@@ -392,10 +390,7 @@ def tile_attngate_kernel(tc, q, k, attention_mask, cos, sin, wq, wk, out):
 
         def rec(n):
             H[n]["rs"] = T(four, [P, 2], F32, "rs")
-            if n < NU - 2:
-                nc.gpsimd.tensor_tensor(out=H[n]["rs"][:], in0=H[n]["ssum"][:], in1=minus1[:], op=ALU.pow)
-            else:
-                nc.vector.reciprocal(out=H[n]["rs"][:], in_=H[n]["ssum"][:])
+            nc.vector.reciprocal(out=H[n]["rs"][:], in_=H[n]["ssum"][:])
 
         def norm(n, cc):
             nc.gpsimd.tensor_scalar(
@@ -418,6 +413,16 @@ def tile_attngate_kernel(tc, q, k, attention_mask, cos, sin, wq, wk, out):
             norm(n, 0)
             norm(n, 1)
             store(n)
+
+        def finish_last(n, cc):
+            h = streams[n // 2][3]
+            if cc == 0:
+                H[n]["rs"] = T(four, [P, 2], F32, "rs")
+            rs, t2 = H[n]["rs"][:, cc:cc + 1], H[n]["t2"][:, cc, :]
+            nc.vector.reciprocal(out=rs, in_=H[n]["ssum"][:, cc:cc + 1])
+            nc.vector.tensor_scalar(out=t2, in0=t2, scalar1=rs, scalar2=None, op0=ALU.mult)
+            rows = slice((n % 2) * HB + cc * P, (n % 2) * HB + (cc + 1) * P)
+            nc.sync.dma_start(out=out[0, h, rows, :], in_=t2)
 
         load(0)
         load_w(0)
@@ -511,7 +516,9 @@ def tile_attngate_kernel(tc, q, k, attention_mask, cos, sin, wq, wk, out):
                 rg_w(3, nc.vector.tensor_copy)
             if t == 3:
                 maskprep()
-                mask_turn()
+                mask_turn((0, 1))
+            if t == 4:
+                mask_turn((2, 3))
 
         last = NU - 1
         mult(last, 0)
@@ -535,7 +542,9 @@ def tile_attngate_kernel(tc, q, k, attention_mask, cos, sin, wq, wk, out):
         softmax_head(last - 1, 1)
         stt(last, 0)
         stt(last, 1)
-        finish(last - 1)
         softmax_head(last, 0)
         softmax_head(last, 1)
-        finish(last)
+        finish_last(last - 1, 0)
+        finish_last(last - 1, 1)
+        finish_last(last, 0)
+        finish_last(last, 1)

import math
from contextlib import ExitStack

import concourse.mybir as mybir
from concourse.masks import make_identity

FP8X4 = mybir.dt.float8_e4m3fn_x4
BF16 = mybir.dt.bfloat16
F32 = mybir.dt.float32
I32 = mybir.dt.int32
U32 = mybir.dt.uint32
U8 = mybir.dt.uint8
ALU = mybir.AluOpType
ACT = mybir.ActivationFunctionType
AX = mybir.AxisListType

P = 128
HQ, HK, S, D, HID, BS = 8, 2, 4096, 256, 512, 8
NB = S // BS
G = HQ // HK
HB = NB // 2
FLOPS = 2 * NB * (2 * D) * HID * (HQ + HK) + 2 * NB * NB * HID * HQ
SCALE = 1.0 / math.sqrt(HID)
PAIRED = (0, 1, 2, 6)


def tile_attngate_kernel(tc, q, k, attention_mask, cos, sin, wq, wk, out):
    nc = tc.nc
    streams = []
    for kv in range(HK):
        streams.append((k[0, kv], wk[kv], kv, None))
        for gq in range(G):
            streams.append((q[0, kv * G + gq], wq[kv * G + gq], kv, kv * G + gq))
    NU = 2 * len(streams)

    with ExitStack() as ctx:
        ctx.enter_context(tc.manual_schedule())
        const = ctx.enter_context(tc.tile_pool(name="const", bufs=1))
        qpool = ctx.enter_context(tc.tile_pool(name="qpool", bufs=5))
        two = ctx.enter_context(tc.tile_pool(name="two", bufs=2))
        three = ctx.enter_context(tc.tile_pool(name="three", bufs=3))
        four = ctx.enter_context(tc.tile_pool(name="four", bufs=4))
        psum = ctx.enter_context(tc.psum_pool(name="psum", bufs=2))
        psum1 = ctx.enter_context(tc.psum_pool(name="psum1", bufs=1))

        H = [dict() for n in range(NU)]
        W = [dict() for s in range(len(streams))]
        YK = []
        for kv in range(HK):
            ykc = const.tile([P, NB], U32, name="ykc%d" % kv, align_bytes=64)
            yks = const.tile([P, NB], U8, name="yks%d" % kv, align_bytes=64)
            YK.append((ykc, yks))

        ident = const.tile([P, P], BF16)
        identf = const.tile([P, P], F32)
        pool32 = const.tile([P, P // BS], F32)
        poolm = const.tile([P, P // BS], BF16)
        pool32b = const.tile([P, P // 4], F32)
        poolm2 = const.tile([P, P // 4], BF16)
        permp = const.tile([P, P], F32)
        cs = const.tile([P, 4, 2, HID], BF16)
        sraw = const.tile([P, 4, D], BF16)
        mbias = const.tile([P, 4, NB], F32)
        mbt = const.tile([P, 4, NB], F32)
        mw = const.tile([P, 4, NB, 2], I32)

        def T(pool, shape, dtype, tag, **kw):
            return pool.tile(shape, dtype, tag=tag, name=tag, **kw)

        def ok(n):
            return 0 <= n < NU

        def isq(n):
            return ok(n) and streams[n // 2][3] is not None

        def paired(n):
            return n // 2 in PAIRED

        def hs_of(n):
            return slice((n % 2) * HB, (n % 2 + 1) * HB)

        def consts():
            make_identity(nc, ident[:])
            make_identity(nc, identf[:])
            nc.vector.tensor_copy(
                out=permp[:].rearrange("p (j b) -> p j b", j=4), in_=identf[:].rearrange("p (b j) -> p j b", j=4)
            )
            nc.vector.tensor_reduce(
                out=pool32b[:], in_=ident[:].rearrange("p (b j) -> p b j", j=4), axis=AX.X, op=ALU.add
            )
            nc.vector.tensor_reduce(
                out=pool32[:], in_=ident[:].rearrange("p (b j) -> p b j", j=BS), axis=AX.X, op=ALU.add
            )
            nc.vector.tensor_scalar(out=poolm2[:], in0=pool32b[:], scalar1=1.0 / BS, scalar2=None, op0=ALU.mult)
            nc.vector.tensor_scalar(out=poolm[:], in0=pool32[:], scalar1=1.0 / BS, scalar2=None, op0=ALU.mult)

        def load_tables(hh):
            c = slice(2 * hh, 2 * hh + 2)
            rows = sin[0].rearrange("(c p) h -> p c h", p=P)
            nc.sync.dma_start(out=cs[:, c, 0, :], in_=cos[0].rearrange("(c p) h -> p c h", p=P)[:, c, :])
            nc.sync.dma_start(out=cs[:, c, 1, 0:D], in_=rows[:, c, D:HID])
            nc.sync.dma_start(out=sraw[:, c, :], in_=rows[:, c, 0:D])
            nc.gpsimd.tensor_scalar(
                out=cs[:, c, 1, D:HID], in0=sraw[:, c, :], scalar1=-1.0, scalar2=0.0, op0=ALU.mult, op1=ALU.add
            )

        def load_mask():
            mi = attention_mask.rearrange("a b i j -> (a b i) j").bitcast(I32)
            nc.sync.dma_start(out=mw[:].rearrange("p c j e -> p c (j e)"), in_=mi.rearrange("(c p) w -> p c w", p=P))

        def maskprep():
            nc.vector.tensor_scalar(
                out=mbias[:], in0=mw[:, :, :, 0], scalar1=-1.0, scalar2=1.0e9, op0=ALU.add, op1=ALU.mult
            )

        def mask_turn(chunks):
            for kc in chunks:
                sc = T(psum, [P, NB], F32, "sc")
                for c in range(4):
                    nc.tensor.matmul(sc[:, c * P:(c + 1) * P], lhsT=mbias[:, c, kc * P:(kc + 1) * P], rhs=identf[:],
                                     is_transpose=True, start=True, stop=True)
                nc.scalar.copy(out=mbt[:, kc, :], in_=sc[:])

        def load(n):
            x = streams[n // 2][0]
            if paired(n):
                q2 = T(qpool, [P, 8, 2, D], BF16, "qp")
                nc.sync.dma_start(
                    out=q2[:].rearrange("p g e f -> p g (e f)"),
                    in_=x.rearrange("(hh g p e) f -> hh p g (e f)", g=8, p=P, e=2)[n % 2],
                )
                H[n]["q2"] = q2
                return
            qa = T(qpool, [P, 2, BS, D], BF16, "qa")
            nc.sync.dma_start(
                out=qa[:].rearrange("p c j f -> p c (j f)"),
                in_=x.rearrange("(hh c p j) f -> hh p c (j f)", c=2, p=P, j=BS)[n % 2],
            )
            qp = T(qpool, [P, 16, D], BF16, "qp")
            nc.sync.dma_start(out=qp[:], in_=x.rearrange("(hh bh p) f -> hh p bh f", p=P, bh=16)[n % 2])
            H[n]["qa"] = qa
            H[n]["qp"] = qp

        def load_w(s):
            wr = T(three, [P, 4, HID], BF16, "wr")
            nc.sync.dma_start(
                out=wr[:].rearrange("p (u e) n -> p u (e n)", u=2),
                in_=streams[s][1].rearrange("(u p e) n -> p u (e n)", u=2, p=P),
            )
            W[s]["wr"] = wr

        def rg_w(j, copy=nc.scalar.copy):
            s = j // 2
            if j % 2 == 0:
                W[s]["wg"] = T(two, [P, HID, 4], BF16, "wg", align_bytes=64)
            copy(
                out=W[s]["wg"][:, hs_of(j), :].rearrange("p (c i) t -> p c t i", i=4),
                in_=W[s]["wr"][:, :, hs_of(j)].rearrange("p t (c i) -> p c t i", i=4),
            )

        def quantise(grouped, codes, scales):
            nc.vector.quantize_mx(
                out=codes.bitcast(FP8X4), scales=scales, in_=grouped[:].rearrange("p n t -> p (n t)")
            )

        def q_w(s):
            W[s]["wc"] = T(two, [P, HID], U32, "wc", align_bytes=64)
            W[s]["ws"] = T(two, [P, HID], U8, "ws", align_bytes=64)
            quantise(W[s]["wg"], W[s]["wc"][:], W[s]["ws"][:])

        def means(n):
            if paired(n):
                mean = T(psum1, [P, 2, HB], F32, "mean")
            else:
                mean = T(psum1, [P, 4, HB], BF16, "mean")
            H[n]["mean"] = mean
            for e in range(2):
                if paired(n):
                    for g in range(8):
                        for r in range(2):
                            nc.tensor.matmul(
                                mean[:, e, g * 32:(g + 1) * 32], lhsT=H[n]["q2"][:, g, r, e::2], rhs=poolm2[:],
                                start=(r == 0), stop=(r == 1),
                            )
                else:
                    for bh in range(16):
                        nc.tensor.matmul(
                            mean[:, e, bh * 16:(bh + 1) * 16], lhsT=H[n]["qp"][:, bh, e::2], rhs=poolm[:],
                            start=True, stop=True,
                        )

        def mevac(n):
            H[n]["z"] = T(three, [P, 2, HB], F32, "z")
            nc.scalar.copy(
                out=H[n]["z"][:, 0, :].bitcast(BF16).rearrange("p (b e) -> p b e", e=2),
                in_=H[n]["mean"][:].rearrange("p e b -> p b e"),
            )

        def max_a(n):
            m1 = T(two, [P, 2, 4, D], BF16, "m1")
            if paired(n):
                q2 = H[n]["q2"]
                nc.vector.tensor_tensor(
                    out=m1[:].rearrange("p c j f -> p (c j) f"), in0=q2[:, :, 0, :], in1=q2[:, :, 1, :], op=ALU.max
                )
            else:
                qa = H[n]["qa"]
                nc.vector.tensor_tensor(out=m1[:], in0=qa[:, :, 0:4, :], in1=qa[:, :, 4:8, :], op=ALU.max)
            H[n]["m1"] = m1

        def turn(n, g4):
            rows = H[n]["m1"][:].rearrange("p c j f -> p (c j) f")
            tw = T(psum1, [P, 4, P], F32, "tw%d" % g4)
            for i in range(4):
                nc.tensor.matmul(tw[:, i, :], lhsT=rows[:, 4 * g4 + i, :].bitcast(F32), rhs=permp[:],
                                 is_transpose=True, start=True, stop=True)
            H[n]["tw%d" % g4] = tw

        def half(n, g4):
            hc = T(two, [P, 4, P // 2], F32, "hc")
            nc.scalar.copy(out=hc[:], in_=H[n]["tw%d" % g4][:, :, P // 2:P])
            H[n]["hc%d" % g4] = hc

        def max_b(n):
            if paired(n):
                H[n]["m2"] = T(two, [P, 8, P], BF16, "mp2")
                for g4 in range(2):
                    tw = H[n]["tw%d" % g4][:].rearrange("p g q -> p (g q)").bitcast(BF16)
                    hc = H[n]["hc%d" % g4][:].rearrange("p g q -> p (g q)").bitcast(BF16)
                    nc.vector.tensor_tensor(
                        out=H[n]["m2"][:, 4 * g4:4 * g4 + 4, :], in0=tw.rearrange("p (g q) -> p g q", g=4)[:, :, 0:P],
                        in1=hc.rearrange("p (g q) -> p g q", g=4), op=ALU.max,
                    )
                return
            m1 = H[n]["m1"]
            m2 = T(two, [P, 2, 2, D], BF16, "mx2")
            nc.vector.tensor_tensor(out=m2[:], in0=m1[:, :, 0:2, :], in1=m1[:, :, 2:4, :], op=ALU.max)
            H[n]["m2"] = m2

        def max_c(n):
            m2 = H[n]["m2"]
            if paired(n):
                nc.vector.tensor_tensor(
                    out=H[n]["z"][:, 1, :].bitcast(BF16).rearrange("p (g q) -> p g q", g=8),
                    in0=m2[:, :, 0:P // 2], in1=m2[:, :, P // 2:P], op=ALU.max,
                )
                return
            m3 = T(two, [P, 2, D], BF16, "m3")
            nc.vector.tensor_tensor(out=m3[:], in0=m2[:, :, 0, :], in1=m2[:, :, 1, :], op=ALU.max)
            H[n]["m3"] = m3

        def turn_max(n):
            for c in range(2):
                for e in range(2):
                    nc.tensor.transpose(
                        H[n]["mean"][:, 2 + e, c * P:(c + 1) * P], H[n]["m3"][:, c, e::2], ident[:]
                    )

        def rg_z(n):
            pg = T(two, [P, HB, 4], BF16, "pg", align_bytes=64)
            if paired(n):
                nc.scalar.copy(
                    out=pg[:].rearrange("p b t -> p (b t)").bitcast(F32).rearrange("p (b s) -> p b s", s=2),
                    in_=H[n]["z"][:].rearrange("p s b -> p b s"),
                )
            else:
                nc.scalar.copy(out=pg[:], in_=H[n]["mean"][:].rearrange("p t b -> p b t"))
            H[n]["pg"] = pg

        def q_p(n):
            H[n]["pc"] = T(two, [P, HB], U32, "pc", align_bytes=64)
            H[n]["ps"] = T(two, [P, HB], U8, "ps", align_bytes=64)
            quantise(H[n]["pg"], H[n]["pc"][:], H[n]["ps"][:])

        def mx(n, cc):
            x = T(psum1, [P, HID], F32, "tw%d" % cc if n == NU - 1 else "x")
            nc.tensor.matmul_mx(
                out=x[:],
                lhsT=H[n]["pc"][:, cc * P:(cc + 1) * P].bitcast(FP8X4), lhsT_scale=H[n]["ps"][:, cc * P:(cc + 1) * P],
                rhs=W[n // 2]["wc"][:].bitcast(FP8X4), rhs_scale=W[n // 2]["ws"][:], start=True, stop=True,
            )
            H[n]["x%d" % cc] = x

        def mult(n, cc):
            ab = T(three, [P, 2, HID], F32, "ab")
            nc.vector.tensor_tensor(
                out=ab[:], in0=H[n]["x%d" % cc][:].unsqueeze(1).to_broadcast([P, 2, HID]),
                in1=cs[:, 2 * (n % 2) + cc], op=ALU.mult,
            )
            H[n]["ab%d" % cc] = ab

        def rope(n, cc):
            ab = H[n]["ab%d" % cc]
            yt = T(psum1, [P, 4, P], F32, "yt")
            for m in range(4):
                mo = (m + 2) % 4
                nc.tensor.matmul(yt[:, m, :], lhsT=ab[:, 0, m * P:(m + 1) * P], rhs=identf[:], is_transpose=True,
                                 start=True, stop=False)
                nc.tensor.matmul(yt[:, m, :], lhsT=ab[:, 1, mo * P:(mo + 1) * P], rhs=identf[:], is_transpose=True,
                                 start=False, stop=True)
            H[n]["yt%d" % cc] = yt

        def yevac(n, cc):
            if cc == 0:
                H[n]["yg"] = T(three, [P, HB, 4], BF16, "yg", align_bytes=64)
            nc.scalar.copy(
                out=H[n]["yg"][:, cc * P:(cc + 1) * P, :], in_=H[n]["yt%d" % cc][:].rearrange("p m b -> p b m")
            )

        def q_y(n):
            kv, h = streams[n // 2][2], streams[n // 2][3]
            if h is None:
                quantise(H[n]["yg"], YK[kv][0][:, hs_of(n)], YK[kv][1][:, hs_of(n)])
            else:
                H[n]["yc"] = T(three, [P, HB], U32, "yc", align_bytes=64)
                H[n]["ys"] = T(three, [P, HB], U8, "ys", align_bytes=64)
                quantise(H[n]["yg"], H[n]["yc"][:], H[n]["ys"][:])

        def score(n, i):
            ykc, yks = YK[streams[n // 2][2]]
            scT = T(psum1, [P, 2, HB], F32, "scT")
            for r in range(2):
                keys = slice((2 * i + r) * P, (2 * i + r + 1) * P)
                nc.tensor.matmul_mx(
                    out=scT[:, r, :], lhsT=ykc[:, keys].bitcast(FP8X4), lhsT_scale=yks[:, keys],
                    rhs=H[n]["yc"][:].bitcast(FP8X4), rhs_scale=H[n]["ys"][:], start=True, stop=True,
                )
            H[n]["scT%d" % i] = scT

        def keep_warm(n):
            idle = T(psum1, [P, NB], F32, "scT")
            w = W[n // 2]
            nc.tensor.matmul_mx(
                out=idle[:], lhsT=w["wc"][:, 0:P].bitcast(FP8X4), lhsT_scale=w["ws"][:, 0:P],
                rhs=w["wc"][:].bitcast(FP8X4), rhs_scale=w["ws"][:], start=True, stop=True,
            )

        def sevac(n, i):
            if i == 0:
                H[n]["st"] = T(two, [P, 4, HB], F32, "st")
            nc.scalar.activation(
                out=H[n]["st"][:, 2 * i:2 * i + 2, :], in_=H[n]["scT%d" % i][:], func=ACT.Copy, scale=SCALE
            )

        def masked(n, cc):
            c = 2 * (n % 2) + cc
            sc = T(psum, [P, NB], F32, "sc")
            for kc in range(4):
                keys = slice(kc * P, (kc + 1) * P)
                nc.tensor.matmul(sc[:, keys], lhsT=H[n]["st"][:, kc, cc * P:(cc + 1) * P], rhs=identf[:],
                                 is_transpose=True, start=True, stop=False)
                nc.tensor.matmul(sc[:, keys], lhsT=mbt[:, kc, c * P:(c + 1) * P], rhs=identf[:],
                                 is_transpose=True, start=False, stop=True)
            H[n]["sc%d" % cc] = sc[:]

        def score_straight(n, cc):
            ykc, yks = YK[streams[n // 2][2]]
            rows = slice(cc * P, (cc + 1) * P)
            sc = T(psum, [P, NB], F32, "sc")
            nc.tensor.matmul_mx(
                out=sc[:], lhsT=H[n]["yc"][:, rows].bitcast(FP8X4), lhsT_scale=H[n]["ys"][:, rows],
                rhs=ykc[:].bitcast(FP8X4), rhs_scale=yks[:], start=True, stop=True,
            )
            H[n]["raw%d" % cc] = sc

        def stt(n, cc):
            if cc == 0:
                H[n]["t1"] = T(three, [P, 2, NB], F32, "ab")
            nc.vector.scalar_tensor_tensor(
                out=H[n]["t1"][:, cc, :], in0=H[n]["raw%d" % cc][:], scalar=SCALE,
                in1=mbias[:, 2 * (n % 2) + cc, :], op0=ALU.mult, op1=ALU.add,
            )
            H[n]["sc%d" % cc] = H[n]["t1"][:, cc, :]

        def red(n, cc):
            if cc == 0:
                H[n]["nmx"] = T(four, [P, 2], F32, "nmx")
            nc.vector.tensor_reduce(
                out=H[n]["nmx"][:, cc:cc + 1], in_=H[n]["sc%d" % cc], axis=AX.X, op=ALU.max, negate=True
            )

        def expo(n, cc):
            if cc == 0:
                H[n]["ssum"] = T(four, [P, 2], F32, "ssum")
                H[n]["t2"] = T(four, [P, 2, NB], F32, "t2")
            nc.scalar.activation(
                out=H[n]["t2"][:, cc, :], in_=H[n]["sc%d" % cc], func=ACT.Exp,
                bias=H[n]["nmx"][:, cc:cc + 1], scale=1.0, accum_out=H[n]["ssum"][:, cc:cc + 1],
            )

        def rec(n):
            H[n]["rs"] = T(four, [P, 2], F32, "rs")
            nc.vector.reciprocal(out=H[n]["rs"][:], in_=H[n]["ssum"][:])

        def norm(n, cc):
            nc.gpsimd.tensor_scalar(
                out=H[n]["t2"][:, cc, :], in0=H[n]["t2"][:, cc, :], scalar1=H[n]["rs"][:, cc:cc + 1], scalar2=1.0,
                op0=ALU.mult, op1=ALU.mult,
            )

        def store(n):
            h = streams[n // 2][3]
            nc.sync.dma_start(
                out=out[0, h, hs_of(n), :].rearrange("(c p) j -> p c j", p=P), in_=H[n]["t2"][:]
            )

        def softmax_head(n, cc):
            red(n, cc)
            expo(n, cc)

        def finish(n):
            rec(n)
            norm(n, 0)
            norm(n, 1)
            store(n)

        def finish_last(n, cc):
            h = streams[n // 2][3]
            if cc == 0:
                H[n]["rs"] = T(four, [P, 2], F32, "rs")
            rs, t2 = H[n]["rs"][:, cc:cc + 1], H[n]["t2"][:, cc, :]
            nc.vector.reciprocal(out=rs, in_=H[n]["ssum"][:, cc:cc + 1])
            nc.vector.tensor_scalar(out=t2, in0=t2, scalar1=rs, scalar2=None, op0=ALU.mult)
            rows = slice((n % 2) * HB + cc * P, (n % 2) * HB + (cc + 1) * P)
            nc.sync.dma_start(out=out[0, h, rows, :], in_=t2)

        load(0)
        load_w(0)
        consts()
        load_tables(0)
        load(1)
        load_tables(1)
        load_w(1)
        load(2)
        load_w(2)
        load(3)
        load_mask()
        for t in range(NU + 1):
            if t % 2 == 1 and (t + 5) // 2 < len(streams):
                load_w((t + 5) // 2)
            if ok(t + 4):
                load(t + 4)
            if ok(t):
                max_a(t)
            if t == 0:
                rg_w(0, nc.vector.tensor_copy)
                rg_w(1, nc.vector.tensor_copy)
            if ok(t) and paired(t):
                turn(t, 0)
                turn(t, 1)
            if ok(t - 1):
                rg_z(t - 1)
            if isq(t - 4):
                red(t - 4, 0)
                expo(t - 4, 0)
            if ok(t) and paired(t):
                half(t, 0)
                half(t, 1)
            if ok(t - 3):
                q_y(t - 3)
            if isq(t - 3):
                score(t - 3, 0)
                sevac(t - 3, 0)
            if ok(t):
                means(t)
            if isq(t - 4):
                red(t - 4, 1)
                expo(t - 4, 1)
            if isq(t - 3):
                score(t - 3, 1)
                sevac(t - 3, 1)
            if ok(t) and paired(t):
                mevac(t)
            if ok(t - 2):
                mult(t - 2, 0)
                mx(t - 2, 1)
                rope(t - 2, 0)
                yevac(t - 2, 0)
            if ok(t - 1):
                q_p(t - 1)
            if t == NU:
                mx(t - 1, 0)
                mx(t - 1, 1)
            if isq(t - 3):
                masked(t - 3, 0)
                if t < NU:
                    keep_warm(t - 2)
            if t > 1 and ok(t + 2):
                rg_w(t + 2)
            if ok(t):
                max_b(t)
            if isq(t - 4):
                rec(t - 4)
                norm(t - 4, 0)
                norm(t - 4, 1)
                store(t - 4)
            if ok(t - 2):
                mult(t - 2, 1)
                rope(t - 2, 1)
            if t % 2 == 0 and t // 2 < len(streams):
                q_w(t // 2)
            if ok(t):
                max_c(t)
                if not paired(t):
                    turn_max(t)
            if isq(t - 3):
                if t < NU:
                    keep_warm(t - 2)
                masked(t - 3, 1)
            if t < NU and ok(t - 1):
                mx(t - 1, 0)
            if ok(t - 2):
                yevac(t - 2, 1)
            if t == 1:
                rg_w(2, nc.vector.tensor_copy)
                rg_w(3, nc.vector.tensor_copy)
            if t == 3:
                maskprep()
                mask_turn((0, 1))
            if t == 4:
                mask_turn((2, 3))

        last = NU - 1
        mult(last, 0)
        rope(last, 0)
        mult(last, 1)
        rope(last, 1)
        yevac(last, 0)
        softmax_head(last - 2, 0)
        q_y(last - 1)
        score_straight(last - 1, 0)
        score_straight(last - 1, 1)
        softmax_head(last - 2, 1)
        yevac(last, 1)
        stt(last - 1, 0)
        stt(last - 1, 1)
        q_y(last)
        score_straight(last, 0)
        score_straight(last, 1)
        finish(last - 2)
        softmax_head(last - 1, 0)
        softmax_head(last - 1, 1)
        stt(last, 0)
        stt(last, 1)
        softmax_head(last, 0)
        softmax_head(last, 1)
        finish_last(last - 1, 0)
        finish_last(last - 1, 1)
        finish_last(last, 0)
        finish_last(last, 1)
